import numpy as np
import ml_dtypes


def mxq(x, axis, fmt="e4m3"):
    dtype, down = {"e4m3": (ml_dtypes.float8_e4m3fn, 7), "e5m2": (ml_dtypes.float8_e5m2, 14)}[fmt]
    v = np.moveaxis(np.asarray(x, np.float32).astype(ml_dtypes.bfloat16).astype(np.float64), axis, -1)
    blocks = v.reshape(v.shape[:-1] + (-1, 32))
    amax = np.abs(blocks).max(-1, keepdims=True)
    byte = np.maximum(np.where(amax > 0, np.frexp(amax)[1] - 1 + 127, 0) - down, 1)
    scale = np.exp2(byte - 127.0)
    codes = (blocks / scale).astype(np.float32).astype(dtype).astype(np.float64)
    return np.moveaxis((codes * scale).reshape(v.shape), -1, axis)


WIDE = False


def mx_kscale(k):
    if not WIDE:
        return np.ones(k)
    levels = np.array([10, -10, 5, -5, 0])
    a = np.random.permutation(np.resize(levels, k // 512 * 4)).reshape(k // 512, 4)
    idx = np.arange(k)
    return np.exp2(a[idx // 512, idx % 128 // 32])


BF16 = ml_dtypes.bfloat16


def bf(x):
    return np.asarray(x, np.float32).astype(BF16)


def f64(x):
    return np.asarray(x).astype(np.float64)


E2M1 = np.array([0.0, 0.5, 1.0, 1.5, 2.0, 3.0, 4.0, 6.0, -0.0, -0.5, -1.0, -1.5, -2.0, -3.0, -4.0, -6.0])


def pack_weight(w, fmt):
    k, n = w.shape
    w = f64(bf(w)).reshape(k // 32, 32, n)
    amax = np.abs(w).max(1)
    if fmt == "e4m3":
        byte = np.frexp(amax)[1] - 1 + 127 - 7
    else:
        mant, ex = np.frexp(amax / 6.0)
        byte = np.where(mant > 0.5, ex, ex - 1) + 127
    byte = np.clip(np.where(amax > 0, byte, 1), 1, 254)
    scaled = (w * np.exp2(127.0 - byte)[:, None, :]).reshape(k, n).astype(np.float32)
    by_word = np.ascontiguousarray(scaled.reshape(k // 512, 128, 4, n).transpose(0, 1, 3, 2))
    if fmt == "e4m3":
        words = by_word.astype(ml_dtypes.float8_e4m3fn).view(np.uint8)
    else:
        c = by_word.astype(ml_dtypes.float4_e2m1fn).view(np.uint8) & 0xF
        words = c[..., 0::2] | (c[..., 1::2] << 4)
    return np.ascontiguousarray(words), np.ascontiguousarray(byte.astype(np.uint8).reshape(k // 512, 16, n))


def unpack_weight(words, scales, fmt):
    g, p, n, _ = words.shape
    if fmt == "e4m3":
        vals = np.ascontiguousarray(words).view(ml_dtypes.float8_e4m3fn).astype(np.float64)
    else:
        nib = np.empty((g, p, n, 4), np.uint8)
        nib[..., 0::2] = words & 0xF
        nib[..., 1::2] = words >> 4
        vals = E2M1[nib]
    vals = vals * np.repeat(np.exp2(scales.astype(np.float64) - 127.0), 8, axis=1)[..., None]
    return vals.transpose(0, 1, 3, 2).reshape(g * 512, n)


B, IN_CH, OUT_CH, KH, KW, H, W_IN = 4, 16, 256, 4, 4, 35, 35
HO, WO = H - KH + 1, W_IN - KW + 1
L = HO * WO
KD = KH * KW
F = IN_CH * KD * KD
MXB = 32
FMT = "e4m3"


def setup_inputs():
    s = mx_kscale(F)[(np.arange(IN_CH) * KD * KD) // MXB * MXB]
    u = np.exp2(np.round(np.log2(s) / 2))
    x = bf(np.random.standard_normal((B, IN_CH, H, W_IN)) * u[None, :, None, None])
    w = np.random.standard_normal((OUT_CH, F)) / np.sqrt(F) / np.repeat(u * u, KD * KD)[None, :]
    words, scales = pack_weight(np.ascontiguousarray(w.T), FMT)
    return {"x": x, "W_words": words, "W_scales": scales}


def _unfold(x):
    patches = np.stack([x[:, :, i:i + HO, j:j + WO] for i in range(KH) for j in range(KW)], axis=2)
    return patches.reshape(B, IN_CH, KD, L).transpose(0, 3, 1, 2)


def reference(x, W_words, W_scales):
    p = _unfold(f64(x))
    outer = np.einsum("blci,blcj->blcij", p, p)
    feat = outer.reshape(B, L, F)
    out = unpack_weight(W_words, W_scales, FMT).T @ mxq(feat, 2, "e4m3").transpose(0, 2, 1)
    return out.reshape(B, OUT_CH, HO, WO)

@@ -1,0 +1,167 @@
+from contextlib import ExitStack
+
+import concourse.mybir as mybir
+
+FLOPS = 2 * 4096 * 4096 * 256
+
+BF16 = mybir.dt.bfloat16
+F32 = mybir.dt.float32
+I32 = mybir.dt.int32
+U8 = mybir.dt.uint8
+U32 = mybir.dt.uint32
+FP8X4 = mybir.dt.float8_e4m3fn_x4
+
+P = 128
+IMAGES = 4
+CHANNELS = 16
+SIDE = 35
+PIXELS = SIDE * SIDE
+GRID = 32
+WINDOW = 4
+OUT_CH = 256
+M_TILE = 128
+N_TILE = 512
+POSITIONS = GRID * GRID
+HALVES = POSITIONS // N_TILE
+PASSES = 8
+COL_GROUPS = GRID // WINDOW
+
+
+def tile_fast2order_de_conv_kernel(tc, x, W_words, W_scales, out):
+    nc = tc.nc
+    with ExitStack() as ctx:
+        keep = ctx.enter_context(tc.tile_pool(name="keep", bufs=1))
+        feat_pool = ctx.enter_context(tc.tile_pool(name="feat", bufs=3))
+        code_pool = ctx.enter_context(tc.tile_pool(name="code", bufs=3))
+        stage_pool = ctx.enter_context(tc.tile_pool(name="stage", bufs=4))
+        psum = ctx.enter_context(tc.psum_pool(name="acc", bufs=2))
+
+        w_words = keep.tile([P, PASSES, OUT_CH * WINDOW], U8, name="w_words", align_bytes=64)
+        w_scales = keep.tile([P, PASSES, OUT_CH], U8, name="w_scales", align_bytes=64)
+        xa = keep.tile([P, IMAGES, PIXELS], BF16, name="xa")
+        xb = keep.tile([P, IMAGES, GRID * SIDE], BF16, name="xb")
+        a_rep = []
+        b_win = []
+        for b in range(IMAGES):
+            a_rep.append(keep.tile([P, 2, SIDE, WINDOW, COL_GROUPS, WINDOW], BF16, name="a_rep%d" % b, align_bytes=64))
+            b_win.append(keep.tile([P, GRID, WINDOW, COL_GROUPS * WINDOW], BF16, name="b_win%d" % b, align_bytes=64))
+
+        nc.vector.memset(w_scales[:].rearrange("p a n -> p (a n)").bitcast(I32), 0)
+
+        x_by_channel = x.rearrange("b c h w -> c b (h w)")
+
+        def load_x(first, count):
+            for icl in range(2):
+                for jr in range(WINDOW):
+                    nc.sync.dma_start(
+                        out=xa[4 * icl + jr : P : 8, first : first + count, 0 : PIXELS - 1],
+                        in_=x_by_channel[:, first : first + count, icl : icl + PIXELS - 1],
+                    )
+            for jr in range(WINDOW):
+                nc.sync.dma_start(
+                    out=xb[jr : P : 8, first : first + count, :],
+                    in_=x_by_channel[:, first : first + count, SIDE * jr : SIDE * jr + GRID * SIDE],
+                )
+            for jr in range(WINDOW):
+                nc.sync.dma_start(
+                    out=xb[4 + jr : P : 8, first : first + count, :],
+                    in_=xb[jr : P : 8, first : first + count, :],
+                )
+
+        load_x(0, 1)
+
+        scale_rows = W_scales.rearrange("g q n -> (g q) n").rearrange("(c a) n -> c (a n)", a=PASSES).bitcast(I32)
+        for quadrant in range(4):
+            nc.sync.dma_start(
+                out=w_scales[32 * quadrant : 32 * quadrant + 4].rearrange("p a n -> p (a n)").bitcast(I32),
+                in_=scale_rows[4 * quadrant : 4 * quadrant + 4, :],
+            )
+        word_rows = W_words.rearrange("g p n t -> (g p) (n t)").bitcast(I32).rearrange("(c a r) w -> a c r w", a=PASSES, r=8)
+        for ich in range(2):
+            for ir in range(WINDOW):
+                a = 2 * ir + ich
+                nc.sync.dma_start(out=w_words[:, a, :].bitcast(I32), in_=word_rows[a])
+
+        load_x(1, IMAGES - 1)
+
+        def expand_a(copy, b, ich, r):
+            rows = xa[:, b, :].rearrange("p (h w) -> p h w", w=SIDE)
+            first = 2 * ich + r
+            picked = rows[:, :, first : first + WINDOW * (COL_GROUPS - 1) + 1 : WINDOW]
+            copy(
+                out=a_rep[b][:, ich, :, r, :, :],
+                in_=picked.unsqueeze(3).to_broadcast([P, SIDE, COL_GROUPS, WINDOW]),
+            )
+
+        def expand_b(copy, b, r):
+            rows = xb[:, b, :].rearrange("p (h w) -> p h w", w=SIDE)
+            copy(out=b_win[b][:, :, r, :], in_=rows[:, :, r : r + GRID])
+
+        for r in range(WINDOW):
+            copy = nc.vector.tensor_copy if r % 2 == 1 else nc.scalar.copy
+            expand_b(copy, 0, r)
+        for r in range(WINDOW):
+            copy = nc.vector.tensor_copy if r % 2 == 1 else nc.scalar.copy
+            expand_a(copy, 0, 0, r)
+        for r in range(WINDOW):
+            expand_a(nc.scalar.copy, 0, 1, r)
+
+        def multiply(b, ich, ir):
+            feat = feat_pool.tile([P, POSITIONS * WINDOW], BF16, name="feat", align_bytes=64)
+            nc.vector.tensor_tensor(
+                out=feat[:],
+                in0=a_rep[b][:, ich, ir : ir + GRID].rearrange("p y r m t -> p (y r m t)"),
+                in1=b_win[b][:].rearrange("p y r k -> p (y r k)"),
+                op=mybir.AluOpType.mult,
+            )
+            return feat
+
+        acc = {}
+
+        def contract(b, ich, ir, feat):
+            codes = code_pool.tile([P, POSITIONS], U32, name="codes", align_bytes=64)
+            scales = code_pool.tile([P, POSITIONS], U8, name="scales", align_bytes=64)
+            nc.vector.quantize_mx(out=codes[:].bitcast(FP8X4), scales=scales[:], in_=feat[:])
+            first = ich == 0 and ir == 0
+            last = ich == 1 and ir == WINDOW - 1
+            a = 2 * ir + ich
+            for oh in range(OUT_CH // M_TILE):
+                for h in range(HALVES):
+                    if first:
+                        acc[(oh, h)] = psum.tile([M_TILE, N_TILE], F32, name="acc%d%d" % (oh, h))
+                    nc.tensor.matmul_mx(
+                        out=acc[(oh, h)][:],
+                        lhsT=w_words[:, a, 4 * M_TILE * oh : 4 * M_TILE * (oh + 1)].bitcast(FP8X4),
+                        lhsT_scale=w_scales[:, a, M_TILE * oh : M_TILE * (oh + 1)],
+                        rhs=codes[:, N_TILE * h : N_TILE * (h + 1)].bitcast(FP8X4),
+                        rhs_scale=scales[:, N_TILE * h : N_TILE * (h + 1)],
+                        start=first,
+                        stop=last,
+                    )
+            if last:
+                rows = GRID // HALVES
+                for oh in range(OUT_CH // M_TILE):
+                    for h in range(HALVES):
+                        stage = stage_pool.tile([M_TILE, rows, COL_GROUPS, WINDOW], F32, name="stage")
+                        nc.scalar.copy(
+                            out=stage[:],
+                            in_=acc[(oh, h)][:].rearrange("p (y r m) -> p y m r", r=WINDOW, m=COL_GROUPS),
+                        )
+                        nc.sync.dma_start(
+                            out=out[b, M_TILE * oh : M_TILE * (oh + 1), rows * h : rows * (h + 1), :].rearrange("o y z -> o (y z)"),
+                            in_=stage[:].rearrange("p y m r -> p (y m r)"),
+                        )
+
+        waiting = None
+        for b in range(IMAGES):
+            for ich in range(2):
+                for ir in range(WINDOW):
+                    if b + 1 < IMAGES:
+                        expand_a(nc.scalar.copy, b + 1, ich, ir)
+                        if ich == 0:
+                            expand_b(nc.scalar.copy, b + 1, ir)
+                    feat = multiply(b, ich, ir)
+                    if waiting is not None:
+                        contract(*waiting)
+                    waiting = (b, ich, ir, feat)
+        contract(*waiting)

@@ -18,119 +18,144 @@ SIDE = 35
 PIXELS = SIDE * SIDE
 GRID = 32
 WINDOW = 4
+COL_GROUPS = GRID // WINDOW
+ROW = GRID * WINDOW
 OUT_CH = 256
 M_TILE = 128
 N_TILE = 512
 POSITIONS = GRID * GRID
 HALVES = POSITIONS // N_TILE
 PASSES = 8
-COL_GROUPS = GRID // WINDOW
+PADDED = SIDE + WINDOW
 
 
 def tile_fast2order_de_conv_kernel(tc, x, W_words, W_scales, out):
     nc = tc.nc
     with ExitStack() as ctx:
+        ctx.enter_context(tc.manual_schedule())
         keep = ctx.enter_context(tc.tile_pool(name="keep", bufs=1))
-        feat_pool = ctx.enter_context(tc.tile_pool(name="feat", bufs=3))
-        code_pool = ctx.enter_context(tc.tile_pool(name="code", bufs=3))
+        prod_pool = ctx.enter_context(tc.tile_pool(name="prod", bufs=2))
+        code_pool = ctx.enter_context(tc.tile_pool(name="code", bufs=4))
         stage_pool = ctx.enter_context(tc.tile_pool(name="stage", bufs=4))
         psum = ctx.enter_context(tc.psum_pool(name="acc", bufs=2))
 
         w_words = keep.tile([P, PASSES, OUT_CH * WINDOW], U8, name="w_words", align_bytes=64)
         w_scales = keep.tile([P, PASSES, OUT_CH], U8, name="w_scales", align_bytes=64)
-        xa = keep.tile([P, IMAGES, PIXELS], BF16, name="xa")
-        xb = keep.tile([P, IMAGES, GRID * SIDE], BF16, name="xb")
-        a_rep = []
-        b_win = []
+        x_left = keep.tile([P, IMAGES, PIXELS], BF16, name="x_left")
+        x_right = keep.tile([P, IMAGES, PADDED, SIDE], BF16, name="x_right")
+        left = []
+        right = []
         for b in range(IMAGES):
-            a_rep.append(keep.tile([P, 2, SIDE, WINDOW, COL_GROUPS, WINDOW], BF16, name="a_rep%d" % b, align_bytes=64))
-            b_win.append(keep.tile([P, GRID, WINDOW, COL_GROUPS * WINDOW], BF16, name="b_win%d" % b, align_bytes=64))
+            left.append(keep.tile([P, 2, SIDE, WINDOW, COL_GROUPS, WINDOW], BF16, name="left%d" % b))
+            right.append(keep.tile([P, PADDED, WINDOW, GRID], BF16, name="right%d" % b))
 
         nc.vector.memset(w_scales[:].rearrange("p a n -> p (a n)").bitcast(I32), 0)
+        nc.vector.memset(x_right[:, :, 0:WINDOW, :], 0)
+        nc.vector.memset(x_right[:, :, SIDE:PADDED, :], 0)
 
         x_by_channel = x.rearrange("b c h w -> c b (h w)")
 
         def load_x(first, count):
             for icl in range(2):
-                for jr in range(WINDOW):
+                for s in range(WINDOW):
                     nc.sync.dma_start(
-                        out=xa[4 * icl + jr : P : 8, first : first + count, 0 : PIXELS - 1],
+                        out=x_left[4 * icl + s : P : 8, first : first + count, 0 : PIXELS - 1],
                         in_=x_by_channel[:, first : first + count, icl : icl + PIXELS - 1],
                     )
-            for jr in range(WINDOW):
-                nc.sync.dma_start(
-                    out=xb[jr : P : 8, first : first + count, :],
-                    in_=x_by_channel[:, first : first + count, SIDE * jr : SIDE * jr + GRID * SIDE],
-                )
-            for jr in range(WINDOW):
-                nc.sync.dma_start(
-                    out=xb[4 + jr : P : 8, first : first + count, :],
-                    in_=xb[jr : P : 8, first : first + count, :],
-                )
+            for icl in range(2):
+                for s in range(WINDOW):
+                    nc.sync.dma_start(
+                        out=x_right[4 * icl + s : P : 8, first : first + count, WINDOW - s : WINDOW - s + SIDE, :].rearrange(
+                            "p b h w -> p b (h w)"
+                        ),
+                        in_=x_by_channel[:, first : first + count, :],
+                    )
+
+        word_rows = (
+            W_words.rearrange("g p n t -> (g p) (n t)")
+            .bitcast(I32)
+            .rearrange("(c a l j) w -> a j c l w", a=PASSES, l=2, j=WINDOW)
+        )
+
+        def load_weights(ich, ir):
+            a = 2 * ir + ich
+            for s in range(WINDOW):
+                nc.sync.dma_start(out=w_words[s:P:WINDOW, a, :].bitcast(I32), in_=word_rows[a, (s + ir) % WINDOW])
 
         load_x(0, 1)
-
         scale_rows = W_scales.rearrange("g q n -> (g q) n").rearrange("(c a) n -> c (a n)", a=PASSES).bitcast(I32)
         for quadrant in range(4):
             nc.sync.dma_start(
                 out=w_scales[32 * quadrant : 32 * quadrant + 4].rearrange("p a n -> p (a n)").bitcast(I32),
                 in_=scale_rows[4 * quadrant : 4 * quadrant + 4, :],
             )
-        word_rows = W_words.rearrange("g p n t -> (g p) (n t)").bitcast(I32).rearrange("(c a r) w -> a c r w", a=PASSES, r=8)
-        for ich in range(2):
-            for ir in range(WINDOW):
-                a = 2 * ir + ich
-                nc.sync.dma_start(out=w_words[:, a, :].bitcast(I32), in_=word_rows[a])
-
+        load_weights(0, 0)
         load_x(1, IMAGES - 1)
+        load_weights(0, 3)
+        load_weights(0, 1)
+        load_weights(0, 2)
 
-        def expand_a(copy, b, ich, r):
-            rows = xa[:, b, :].rearrange("p (h w) -> p h w", w=SIDE)
+        def expand_left(copy, b, ich, r):
+            rows = x_left[:, b, :].rearrange("p (h w) -> p h w", w=SIDE)
             first = 2 * ich + r
             picked = rows[:, :, first : first + WINDOW * (COL_GROUPS - 1) + 1 : WINDOW]
             copy(
-                out=a_rep[b][:, ich, :, r, :, :],
+                out=left[b][:, ich, :, r, :, :],
                 in_=picked.unsqueeze(3).to_broadcast([P, SIDE, COL_GROUPS, WINDOW]),
             )
 
-        def expand_b(copy, b, r):
-            rows = xb[:, b, :].rearrange("p (h w) -> p h w", w=SIDE)
-            copy(out=b_win[b][:, :, r, :], in_=rows[:, :, r : r + GRID])
+        def expand_right(copy, b, r):
+            copy(out=right[b][:, :, r, :], in_=x_right[:, b, :, r : r + GRID])
 
         for r in range(WINDOW):
-            copy = nc.vector.tensor_copy if r % 2 == 1 else nc.scalar.copy
-            expand_b(copy, 0, r)
+            expand_right(nc.vector.tensor_copy, 0, r)
         for r in range(WINDOW):
-            copy = nc.vector.tensor_copy if r % 2 == 1 else nc.scalar.copy
-            expand_a(copy, 0, 0, r)
+            expand_left(nc.vector.tensor_copy if r >= 2 else nc.scalar.copy, 0, 0, r)
         for r in range(WINDOW):
-            expand_a(nc.scalar.copy, 0, 1, r)
+            expand_left(nc.scalar.copy, 0, 1, r)
 
-        def multiply(b, ich, ir):
-            feat = feat_pool.tile([P, POSITIONS * WINDOW], BF16, name="feat", align_bytes=64)
-            nc.vector.tensor_tensor(
-                out=feat[:],
-                in0=a_rep[b][:, ich, ir : ir + GRID].rearrange("p y r m t -> p (y r m t)"),
-                in1=b_win[b][:].rearrange("p y r k -> p (y r k)"),
-                op=mybir.AluOpType.mult,
-            )
-            return feat
-
+        below = {}
+        above = {}
         acc = {}
 
-        def contract(b, ich, ir, feat):
+        def lane(tile_ap, s, first_row, last_row):
+            return tile_ap[s:P:WINDOW, first_row : last_row + 1, :]
+
+        def multiply_below(b, ich):
+            below[(b, ich)] = prod_pool.tile([P, SIDE, ROW], BF16, name="below", align_bytes=64)
+            nc.vector.tensor_tensor(
+                out=below[(b, ich)][:].rearrange("p u k -> p (u k)"),
+                in0=left[b][:, ich].rearrange("p u r m t -> p (u r m t)"),
+                in1=right[b][:, WINDOW:PADDED].rearrange("p w r k -> p (w r k)"),
+                op=mybir.AluOpType.mult,
+            )
+
+        def multiply_above(b, ich):
+            above[(b, ich)] = prod_pool.tile([P, SIDE, ROW], BF16, name="above", align_bytes=64)
+            nc.vector.tensor_tensor(
+                out=above[(b, ich)][:, 1:SIDE].rearrange("p u k -> p (u k)"),
+                in0=left[b][:, ich, 1:SIDE].rearrange("p u r m t -> p (u r m t)"),
+                in1=right[b][:, 1:SIDE].rearrange("p w r k -> p (w r k)"),
+                op=mybir.AluOpType.mult,
+            )
+
+        def contract(b, ich, ir, products):
             codes = code_pool.tile([P, POSITIONS], U32, name="codes", align_bytes=64)
             scales = code_pool.tile([P, POSITIONS], U8, name="scales", align_bytes=64)
-            nc.vector.quantize_mx(out=codes[:].bitcast(FP8X4), scales=scales[:], in_=feat[:])
+            nc.vector.quantize_mx(
+                out=codes[:].bitcast(FP8X4),
+                scales=scales[:],
+                in_=products[:, ir : ir + GRID].rearrange("p u k -> p (u k)"),
+            )
             first = ich == 0 and ir == 0
-            last = ich == 1 and ir == WINDOW - 1
+            last = ich == 1 and ir == 2
             a = 2 * ir + ich
             for oh in range(OUT_CH // M_TILE):
                 for h in range(HALVES):
                     if first:
-                        acc[(oh, h)] = psum.tile([M_TILE, N_TILE], F32, name="acc%d%d" % (oh, h))
+                        acc[(b, oh, h)] = psum.tile([M_TILE, N_TILE], F32, name="acc%d%d" % (oh, h))
                     nc.tensor.matmul_mx(
-                        out=acc[(oh, h)][:],
+                        out=acc[(b, oh, h)][:],
                         lhsT=w_words[:, a, 4 * M_TILE * oh : 4 * M_TILE * (oh + 1)].bitcast(FP8X4),
                         lhsT_scale=w_scales[:, a, M_TILE * oh : M_TILE * (oh + 1)],
                         rhs=codes[:, N_TILE * h : N_TILE * (h + 1)].bitcast(FP8X4),
@@ -143,25 +168,43 @@ def tile_fast2order_de_conv_kernel(tc, x, W_words, W_scales, out):
                 for oh in range(OUT_CH // M_TILE):
                     for h in range(HALVES):
                         stage = stage_pool.tile([M_TILE, rows, COL_GROUPS, WINDOW], F32, name="stage")
-                        nc.scalar.copy(
+                        copy = nc.vector.tensor_copy if b == IMAGES - 1 and oh == 1 else nc.scalar.copy
+                        copy(
                             out=stage[:],
-                            in_=acc[(oh, h)][:].rearrange("p (y r m) -> p y m r", r=WINDOW, m=COL_GROUPS),
+                            in_=acc[(b, oh, h)][:].rearrange("p (y r m) -> p y m r", r=WINDOW, m=COL_GROUPS),
                         )
                         nc.sync.dma_start(
-                            out=out[b, M_TILE * oh : M_TILE * (oh + 1), rows * h : rows * (h + 1), :].rearrange("o y z -> o (y z)"),
+                            out=out[b, M_TILE * oh : M_TILE * (oh + 1), rows * h : rows * (h + 1), :].rearrange(
+                                "o y z -> o (y z)"
+                            ),
                             in_=stage[:].rearrange("p y m r -> p (y m r)"),
                         )
 
-        waiting = None
-        for b in range(IMAGES):
-            for ich in range(2):
-                for ir in range(WINDOW):
-                    if b + 1 < IMAGES:
-                        expand_a(nc.scalar.copy, b + 1, ich, ir)
-                        if ich == 0:
-                            expand_b(nc.scalar.copy, b + 1, ir)
-                    feat = multiply(b, ich, ir)
-                    if waiting is not None:
-                        contract(*waiting)
-                    waiting = (b, ich, ir, feat)
-        contract(*waiting)
+        groups = [(b, ich) for b in range(IMAGES) for ich in range(2)]
+        for k in range(len(groups) + 1):
+            new = groups[k] if k < len(groups) else None
+            old = groups[k - 1] if k > 0 else None
+            if new is not None:
+                b, ich = new
+                if b + 1 < IMAGES:
+                    for r in range(WINDOW):
+                        expand_left(nc.scalar.copy, b + 1, ich, r)
+                    expand_right(nc.scalar.copy, b + 1, 2 * ich)
+                    expand_right(nc.scalar.copy, b + 1, 2 * ich + 1)
+                multiply_below(b, ich)
+            if old is not None:
+                contract(old[0], old[1], 3, above[old])
+                nc.sync.dma_start(out=lane(above[old], 1, 2, GRID + 1), in_=lane(below[old], 1, 2, GRID + 1))
+            if new is not None:
+                multiply_above(new[0], new[1])
+                nc.sync.dma_start(out=lane(above[new], 0, 2, SIDE - 1), in_=lane(below[new], 0, 2, SIDE - 1))
+            if old is not None:
+                contract(old[0], old[1], 1, below[old])
+            if new is not None:
+                contract(new[0], new[1], 0, below[new])
+                nc.sync.dma_start(out=lane(below[new], 3, 1, GRID), in_=lane(above[new], 3, 1, GRID))
+                if k == 0:
+                    for ir in (0, 3, 1, 2):
+                        load_weights(1, ir)
+            if old is not None:
+                contract(old[0], old[1], 2, above[old])

@@ -19,7 +19,7 @@ PIXELS = SIDE * SIDE
 GRID = 32
 WINDOW = 4
 COL_GROUPS = GRID // WINDOW
-ROW = GRID * WINDOW
+LEFT_GROUPS = 12
 OUT_CH = 256
 M_TILE = 128
 N_TILE = 512
@@ -41,35 +41,34 @@ def tile_fast2order_de_conv_kernel(tc, x, W_words, W_scales, out):
 
         w_words = keep.tile([P, PASSES, OUT_CH * WINDOW], U8, name="w_words", align_bytes=64)
         w_scales = keep.tile([P, PASSES, OUT_CH], U8, name="w_scales", align_bytes=64)
-        x_left = keep.tile([P, IMAGES, PIXELS], BF16, name="x_left")
-        x_right = keep.tile([P, IMAGES, PADDED, SIDE], BF16, name="x_right")
+        x_left = []
+        x_right = []
         left = []
         right = []
         for b in range(IMAGES):
-            left.append(keep.tile([P, 2, SIDE, WINDOW, COL_GROUPS, WINDOW], BF16, name="left%d" % b))
+            x_left.append(keep.tile([P, PIXELS], BF16, name="x_left%d" % b))
+            x_right.append(keep.tile([P, PADDED, SIDE], BF16, name="x_right%d" % b))
+            left.append(keep.tile([P, SIDE, WINDOW, LEFT_GROUPS, WINDOW], BF16, name="left%d" % b))
             right.append(keep.tile([P, PADDED, WINDOW, GRID], BF16, name="right%d" % b))
 
         nc.vector.memset(w_scales[:].rearrange("p a n -> p (a n)").bitcast(I32), 0)
-        nc.vector.memset(x_right[:, :, 0:WINDOW, :], 0)
-        nc.vector.memset(x_right[:, :, SIDE:PADDED, :], 0)
+        for b in range(IMAGES):
+            nc.gpsimd.memset(x_right[b][:, 0:WINDOW, :], 0)
+            nc.gpsimd.memset(x_right[b][:, SIDE:PADDED, :], 0)
 
-        x_by_channel = x.rearrange("b c h w -> c b (h w)")
-
-        def load_x(first, count):
+        def load_x(b):
+            pixels = x[b].rearrange("c h w -> c (h w)")
             for icl in range(2):
                 for s in range(WINDOW):
                     nc.sync.dma_start(
-                        out=x_left[4 * icl + s : P : 8, first : first + count, 0 : PIXELS - 1],
-                        in_=x_by_channel[:, first : first + count, icl : icl + PIXELS - 1],
+                        out=x_left[b][4 * icl + s : P : 8, 0 : PIXELS - 1],
+                        in_=pixels[:, icl : icl + PIXELS - 1],
                     )
-            for icl in range(2):
-                for s in range(WINDOW):
-                    nc.sync.dma_start(
-                        out=x_right[4 * icl + s : P : 8, first : first + count, WINDOW - s : WINDOW - s + SIDE, :].rearrange(
-                            "p b h w -> p b (h w)"
-                        ),
-                        in_=x_by_channel[:, first : first + count, :],
-                    )
+            for s in range(WINDOW):
+                nc.sync.dma_start(
+                    out=x_right[b][s:P:WINDOW, WINDOW - s : WINDOW - s + SIDE, :].rearrange("p h w -> p (h w)"),
+                    in_=pixels.unsqueeze(1).to_broadcast([CHANNELS, 2, PIXELS]),
+                )
 
         word_rows = (
             W_words.rearrange("g p n t -> (g p) (n t)")
@@ -82,7 +81,26 @@ def tile_fast2order_de_conv_kernel(tc, x, W_words, W_scales, out):
             for s in range(WINDOW):
                 nc.sync.dma_start(out=w_words[s:P:WINDOW, a, :].bitcast(I32), in_=word_rows[a, (s + ir) % WINDOW])
 
-        load_x(0, 1)
+        def expand_left(copy, b, r):
+            groups_here = COL_GROUPS + 1 if r < 2 else COL_GROUPS
+            rows = x_left[b][:].rearrange("p (h w) -> p h w", w=SIDE)
+            picked = rows[:, :, r : r + WINDOW * (groups_here - 1) + 1 : WINDOW]
+            copy(
+                out=left[b][:, :, r, 0:groups_here, :],
+                in_=picked.unsqueeze(3).to_broadcast([P, SIDE, groups_here, WINDOW]),
+            )
+
+        def expand_right(copy, b, r):
+            copy(out=right[b][:, :, r, :], in_=x_right[b][:, :, r : r + GRID])
+
+        load_x(0)
+        expand_left(nc.scalar.copy, 0, 0)
+        expand_left(nc.scalar.copy, 0, 1)
+        expand_left(nc.vector.tensor_copy, 0, 2)
+        expand_left(nc.vector.tensor_copy, 0, 3)
+        for r in range(WINDOW):
+            expand_right(nc.vector.tensor_copy, 0, r)
+
         scale_rows = W_scales.rearrange("g q n -> (g q) n").rearrange("(c a) n -> c (a n)", a=PASSES).bitcast(I32)
         for quadrant in range(4):
             nc.sync.dma_start(
@@ -90,54 +108,32 @@ def tile_fast2order_de_conv_kernel(tc, x, W_words, W_scales, out):
                 in_=scale_rows[4 * quadrant : 4 * quadrant + 4, :],
             )
         load_weights(0, 0)
-        load_x(1, IMAGES - 1)
+        load_x(1)
         load_weights(0, 3)
         load_weights(0, 1)
         load_weights(0, 2)
-
-        def expand_left(copy, b, ich, r):
-            rows = x_left[:, b, :].rearrange("p (h w) -> p h w", w=SIDE)
-            first = 2 * ich + r
-            picked = rows[:, :, first : first + WINDOW * (COL_GROUPS - 1) + 1 : WINDOW]
-            copy(
-                out=left[b][:, ich, :, r, :, :],
-                in_=picked.unsqueeze(3).to_broadcast([P, SIDE, COL_GROUPS, WINDOW]),
-            )
-
-        def expand_right(copy, b, r):
-            copy(out=right[b][:, :, r, :], in_=x_right[:, b, :, r : r + GRID])
-
-        for r in range(WINDOW):
-            expand_right(nc.vector.tensor_copy, 0, r)
-        for r in range(WINDOW):
-            expand_left(nc.vector.tensor_copy if r >= 2 else nc.scalar.copy, 0, 0, r)
-        for r in range(WINDOW):
-            expand_left(nc.scalar.copy, 0, 1, r)
 
         below = {}
         above = {}
         acc = {}
 
-        def lane(tile_ap, s, first_row, last_row):
-            return tile_ap[s:P:WINDOW, first_row : last_row + 1, :]
+        def lane(products, s, first_row, last_row):
+            return products[s:P:WINDOW, first_row : last_row + 1]
 
-        def multiply_below(b, ich):
-            below[(b, ich)] = prod_pool.tile([P, SIDE, ROW], BF16, name="below", align_bytes=64)
-            nc.vector.tensor_tensor(
-                out=below[(b, ich)][:].rearrange("p u k -> p (u k)"),
-                in0=left[b][:, ich].rearrange("p u r m t -> p (u r m t)"),
-                in1=right[b][:, WINDOW:PADDED].rearrange("p w r k -> p (w r k)"),
-                op=mybir.AluOpType.mult,
-            )
-
-        def multiply_above(b, ich):
-            above[(b, ich)] = prod_pool.tile([P, SIDE, ROW], BF16, name="above", align_bytes=64)
-            nc.vector.tensor_tensor(
-                out=above[(b, ich)][:, 1:SIDE].rearrange("p u k -> p (u k)"),
-                in0=left[b][:, ich, 1:SIDE].rearrange("p u r m t -> p (u r m t)"),
-                in1=right[b][:, 1:SIDE].rearrange("p w r k -> p (w r k)"),
-                op=mybir.AluOpType.mult,
-            )
+        def multiply(products, b, ich, first_row, right_shift):
+            shift = 2 * ich
+            parts = [(0, WINDOW - shift, shift, 0)]
+            if shift > 0:
+                parts.append((WINDOW - shift, shift, 0, 1))
+            for r, count, left_r, left_m in parts:
+                nc.vector.tensor_tensor(
+                    out=products[:, first_row:SIDE, r : r + count, :],
+                    in0=left[b][:, first_row:SIDE, left_r : left_r + count, left_m : left_m + COL_GROUPS, :].rearrange(
+                        "p u r m t -> p u r (m t)"
+                    ),
+                    in1=right[b][:, first_row + right_shift : SIDE + right_shift, r : r + count, :],
+                    op=mybir.AluOpType.mult,
+                )
 
         def contract(b, ich, ir, products):
             codes = code_pool.tile([P, POSITIONS], U32, name="codes", align_bytes=64)
@@ -145,7 +141,7 @@ def tile_fast2order_de_conv_kernel(tc, x, W_words, W_scales, out):
             nc.vector.quantize_mx(
                 out=codes[:].bitcast(FP8X4),
                 scales=scales[:],
-                in_=products[:, ir : ir + GRID].rearrange("p u k -> p (u k)"),
+                in_=products[:, ir : ir + GRID].rearrange("p u r k -> p (u r k)"),
             )
             first = ich == 0 and ir == 0
             last = ich == 1 and ir == 2
@@ -188,15 +184,18 @@ def tile_fast2order_de_conv_kernel(tc, x, W_words, W_scales, out):
                 b, ich = new
                 if b + 1 < IMAGES:
                     for r in range(WINDOW):
-                        expand_left(nc.scalar.copy, b + 1, ich, r)
-                    expand_right(nc.scalar.copy, b + 1, 2 * ich)
-                    expand_right(nc.scalar.copy, b + 1, 2 * ich + 1)
-                multiply_below(b, ich)
+                        if ich == 0:
+                            expand_left(nc.scalar.copy, b + 1, r)
+                        else:
+                            expand_right(nc.scalar.copy, b + 1, r)
+                below[new] = prod_pool.tile([P, SIDE, WINDOW, GRID], BF16, name="below", align_bytes=64)
+                multiply(below[new], b, ich, 0, WINDOW)
             if old is not None:
                 contract(old[0], old[1], 3, above[old])
                 nc.sync.dma_start(out=lane(above[old], 1, 2, GRID + 1), in_=lane(below[old], 1, 2, GRID + 1))
             if new is not None:
-                multiply_above(new[0], new[1])
+                above[new] = prod_pool.tile([P, SIDE, WINDOW, GRID], BF16, name="above", align_bytes=64)
+                multiply(above[new], new[0], new[1], 1, 0)
                 nc.sync.dma_start(out=lane(above[new], 0, 2, SIDE - 1), in_=lane(below[new], 0, 2, SIDE - 1))
             if old is not None:
                 contract(old[0], old[1], 1, below[old])
@@ -206,5 +205,7 @@ def tile_fast2order_de_conv_kernel(tc, x, W_words, W_scales, out):
                 if k == 0:
                     for ir in (0, 3, 1, 2):
                         load_weights(1, ir)
+                if new[1] == 0 and new[0] + 2 < IMAGES:
+                    load_x(new[0] + 2)
             if old is not None:
                 contract(old[0], old[1], 2, above[old])

@@ -44,12 +44,10 @@ def tile_fast2order_de_conv_kernel(tc, x, W_words, W_scales, out):
         x_left = []
         x_right = []
         left = []
-        right = []
         for b in range(IMAGES):
             x_left.append(keep.tile([P, PIXELS], BF16, name="x_left%d" % b))
             x_right.append(keep.tile([P, PADDED, SIDE], BF16, name="x_right%d" % b))
             left.append(keep.tile([P, SIDE, WINDOW, LEFT_GROUPS, WINDOW], BF16, name="left%d" % b))
-            right.append(keep.tile([P, PADDED, WINDOW, GRID], BF16, name="right%d" % b))
 
         nc.vector.memset(w_scales[:].rearrange("p a n -> p (a n)").bitcast(I32), 0)
         for b in range(IMAGES):
@@ -90,16 +88,11 @@ def tile_fast2order_de_conv_kernel(tc, x, W_words, W_scales, out):
                 in_=picked.unsqueeze(3).to_broadcast([P, SIDE, groups_here, WINDOW]),
             )
 
-        def expand_right(copy, b, r):
-            copy(out=right[b][:, :, r, :], in_=x_right[b][:, :, r : r + GRID])
-
         load_x(0)
         expand_left(nc.scalar.copy, 0, 0)
         expand_left(nc.scalar.copy, 0, 1)
         expand_left(nc.vector.tensor_copy, 0, 2)
         expand_left(nc.vector.tensor_copy, 0, 3)
-        for r in range(WINDOW):
-            expand_right(nc.vector.tensor_copy, 0, r)
 
         scale_rows = W_scales.rearrange("g q n -> (g q) n").rearrange("(c a) n -> c (a n)", a=PASSES).bitcast(I32)
         for quadrant in range(4):
@@ -122,16 +115,14 @@ def tile_fast2order_de_conv_kernel(tc, x, W_words, W_scales, out):
 
         def multiply(products, b, ich, first_row, right_shift):
             shift = 2 * ich
-            parts = [(0, WINDOW - shift, shift, 0)]
-            if shift > 0:
-                parts.append((WINDOW - shift, shift, 0, 1))
-            for r, count, left_r, left_m in parts:
+            for r in range(WINDOW):
+                left_m, left_r = divmod(r + shift, WINDOW)
                 nc.vector.tensor_tensor(
-                    out=products[:, first_row:SIDE, r : r + count, :],
-                    in0=left[b][:, first_row:SIDE, left_r : left_r + count, left_m : left_m + COL_GROUPS, :].rearrange(
-                        "p u r m t -> p u r (m t)"
+                    out=products[:, first_row:SIDE, r, :],
+                    in0=left[b][:, first_row:SIDE, left_r, left_m : left_m + COL_GROUPS, :].rearrange(
+                        "p u m t -> p u (m t)"
                     ),
-                    in1=right[b][:, first_row + right_shift : SIDE + right_shift, r : r + count, :],
+                    in1=x_right[b][:, first_row + right_shift : SIDE + right_shift, r : r + GRID],
                     op=mybir.AluOpType.mult,
                 )
 
@@ -186,8 +177,6 @@ def tile_fast2order_de_conv_kernel(tc, x, W_words, W_scales, out):
                     for r in range(WINDOW):
                         if ich == 0:
                             expand_left(nc.scalar.copy, b + 1, r)
-                        else:
-                            expand_right(nc.scalar.copy, b + 1, r)
                 below[new] = prod_pool.tile([P, SIDE, WINDOW, GRID], BF16, name="below", align_bytes=64)
                 multiply(below[new], b, ich, 0, WINDOW)
             if old is not None:

@@ -13,6 +13,7 @@ FP8X4 = mybir.dt.float8_e4m3fn_x4
 
 P = 128
 IMAGES = 4
+LAST = IMAGES - 1
 CHANNELS = 16
 SIDE = 35
 PIXELS = SIDE * SIDE
@@ -25,8 +26,8 @@ M_TILE = 128
 N_TILE = 512
 POSITIONS = GRID * GRID
 HALVES = POSITIONS // N_TILE
+ABOVE_ROWS = SIDE + WINDOW - 1
 PASSES = 8
-PADDED = SIDE + WINDOW
 
 
 def tile_fast2order_de_conv_kernel(tc, x, W_words, W_scales, out):
@@ -34,7 +35,9 @@ def tile_fast2order_de_conv_kernel(tc, x, W_words, W_scales, out):
     with ExitStack() as ctx:
         ctx.enter_context(tc.manual_schedule())
         keep = ctx.enter_context(tc.tile_pool(name="keep", bufs=1))
-        prod_pool = ctx.enter_context(tc.tile_pool(name="prod", bufs=2))
+        left_pool = ctx.enter_context(tc.tile_pool(name="left", bufs=2))
+        below_pool = ctx.enter_context(tc.tile_pool(name="below", bufs=4))
+        above_pool = ctx.enter_context(tc.tile_pool(name="above", bufs=3))
         code_pool = ctx.enter_context(tc.tile_pool(name="code", bufs=4))
         stage_pool = ctx.enter_context(tc.tile_pool(name="stage", bufs=4))
         psum = ctx.enter_context(tc.psum_pool(name="acc", bufs=2))
@@ -42,89 +45,128 @@ def tile_fast2order_de_conv_kernel(tc, x, W_words, W_scales, out):
         w_words = keep.tile([P, PASSES, OUT_CH * WINDOW], U8, name="w_words", align_bytes=64)
         w_scales = keep.tile([P, PASSES, OUT_CH], U8, name="w_scales", align_bytes=64)
         x_left = []
-        x_right = []
-        left = []
+        x_below = []
+        x_above = []
         for b in range(IMAGES):
             x_left.append(keep.tile([P, PIXELS], BF16, name="x_left%d" % b))
-            x_right.append(keep.tile([P, PADDED, SIDE], BF16, name="x_right%d" % b))
-            left.append(keep.tile([P, SIDE, WINDOW, LEFT_GROUPS, WINDOW], BF16, name="left%d" % b))
+            x_below.append(keep.tile([P, SIDE, SIDE], BF16, name="x_below%d" % b))
+            if b < LAST:
+                x_above.append(keep.tile([P, ABOVE_ROWS, SIDE], BF16, name="x_above%d" % b))
+        x_left_above0 = keep.tile([P, PIXELS], BF16, name="x_left_above0")
 
         nc.vector.memset(w_scales[:].rearrange("p a n -> p (a n)").bitcast(I32), 0)
         for b in range(IMAGES):
-            nc.gpsimd.memset(x_right[b][:, 0:WINDOW, :], 0)
-            nc.gpsimd.memset(x_right[b][:, SIDE:PADDED, :], 0)
+            nc.gpsimd.memset(x_below[b][:, SIDE - WINDOW + 1 : SIDE, :], 0)
+            if b < LAST:
+                nc.gpsimd.memset(x_above[b][:, 0 : WINDOW - 1, :], 0)
+
+        pixels = x.rearrange("b c h w -> b c (h w)")
+
+        def load_left_lane(tile, source, s):
+            for icl in range(2):
+                nc.sync.dma_start(
+                    out=tile[4 * icl + s : P : 8, 0 : PIXELS - 1],
+                    in_=pixels[source, :, icl : icl + PIXELS - 1],
+                )
+
+        def load_rows(tile, source, s, image_row, tile_row, count):
+            nc.sync.dma_start(
+                out=tile[s:P:WINDOW, tile_row : tile_row + count, :].rearrange("p h w -> p (h w)"),
+                in_=pixels[source, :, image_row * SIDE : (image_row + count) * SIDE]
+                .unsqueeze(1)
+                .to_broadcast([CHANNELS, 2, count * SIDE]),
+            )
 
         def load_x(b):
-            pixels = x[b].rearrange("c h w -> c (h w)")
-            for icl in range(2):
-                for s in range(WINDOW):
-                    nc.sync.dma_start(
-                        out=x_left[b][4 * icl + s : P : 8, 0 : PIXELS - 1],
-                        in_=pixels[:, icl : icl + PIXELS - 1],
-                    )
             for s in range(WINDOW):
-                nc.sync.dma_start(
-                    out=x_right[b][s:P:WINDOW, WINDOW - s : WINDOW - s + SIDE, :].rearrange("p h w -> p (h w)"),
-                    in_=pixels.unsqueeze(1).to_broadcast([CHANNELS, 2, PIXELS]),
-                )
+                load_left_lane(x_left[b], b, s)
+            for s in range(WINDOW):
+                load_rows(x_below[b], b, s, s, 0, SIDE - s)
+
+        def load_x_above(b):
+            for s in range(WINDOW):
+                drop = WINDOW - s if s > 0 else LAST - b
+                load_rows(x_above[b], b if s > 0 else LAST, s, 0, drop, SIDE)
+
+        def prepare_above(b):
+            load_left_lane(x_left[b], LAST, 0)
+            load_x_above(b)
 
         word_rows = (
             W_words.rearrange("g p n t -> (g p) (n t)")
             .bitcast(I32)
             .rearrange("(c a l j) w -> a j c l w", a=PASSES, l=2, j=WINDOW)
         )
+        word_rows_in_order = (
+            W_words.rearrange("g p n t -> (g p) (n t)").bitcast(I32).rearrange("(c a q) w -> a c q w", a=PASSES, q=8)
+        )
 
         def load_weights(ich, ir):
             a = 2 * ir + ich
-            for s in range(WINDOW):
-                nc.sync.dma_start(out=w_words[s:P:WINDOW, a, :].bitcast(I32), in_=word_rows[a, (s + ir) % WINDOW])
+            if ir == 0:
+                nc.sync.dma_start(out=w_words[:, a, :].bitcast(I32), in_=word_rows_in_order[a])
+            else:
+                for s in range(WINDOW):
+                    nc.sync.dma_start(
+                        out=w_words[s:P:WINDOW, a, :].bitcast(I32), in_=word_rows[a, (s + ir) % WINDOW]
+                    )
 
-        def expand_left(copy, b, r):
+        def expand_left(copy, tile, source, r, first_row):
             groups_here = COL_GROUPS + 1 if r < 2 else COL_GROUPS
-            rows = x_left[b][:].rearrange("p (h w) -> p h w", w=SIDE)
-            picked = rows[:, :, r : r + WINDOW * (groups_here - 1) + 1 : WINDOW]
+            rows = source[:].rearrange("p (h w) -> p h w", w=SIDE)
+            picked = rows[:, first_row:SIDE, r : r + WINDOW * (groups_here - 1) + 1 : WINDOW]
             copy(
-                out=left[b][:, :, r, 0:groups_here, :],
-                in_=picked.unsqueeze(3).to_broadcast([P, SIDE, groups_here, WINDOW]),
+                out=tile[:, first_row:SIDE, r, 0:groups_here, :],
+                in_=picked.unsqueeze(3).to_broadcast([P, SIDE - first_row, groups_here, WINDOW]),
             )
 
-        load_x(0)
-        expand_left(nc.scalar.copy, 0, 0)
-        expand_left(nc.scalar.copy, 0, 1)
-        expand_left(nc.vector.tensor_copy, 0, 2)
-        expand_left(nc.vector.tensor_copy, 0, 3)
+        left_below = {}
+        left_above = {}
 
-        scale_rows = W_scales.rearrange("g q n -> (g q) n").rearrange("(c a) n -> c (a n)", a=PASSES).bitcast(I32)
-        for quadrant in range(4):
-            nc.sync.dma_start(
-                out=w_scales[32 * quadrant : 32 * quadrant + 4].rearrange("p a n -> p (a n)").bitcast(I32),
-                in_=scale_rows[4 * quadrant : 4 * quadrant + 4, :],
-            )
-        load_weights(0, 0)
-        load_x(1)
-        load_weights(0, 3)
-        load_weights(0, 1)
-        load_weights(0, 2)
+        def new_left(name):
+            return left_pool.tile([P, SIDE, WINDOW, LEFT_GROUPS, WINDOW], BF16, name=name)
+
+        def expand_below(b):
+            left_below[b] = new_left("left_below")
+            for r in range(WINDOW):
+                expand_left(nc.scalar.copy, left_below[b], x_left[b], r, 0)
+
+        def expand_above(b, source):
+            left_above[b] = new_left("left_above")
+            for r in range(WINDOW):
+                expand_left(nc.scalar.copy, left_above[b], source, r, 1)
 
         below = {}
         above = {}
         acc = {}
+        opened = set()
 
         def lane(products, s, first_row, last_row):
             return products[s:P:WINDOW, first_row : last_row + 1]
 
-        def multiply(products, b, ich, first_row, right_shift):
-            shift = 2 * ich
-            for r in range(WINDOW):
-                left_m, left_r = divmod(r + shift, WINDOW)
+        def multiply(products, left, right, ich, first_row, r_order):
+            for r in r_order:
+                left_m, left_r = divmod(r + 2 * ich, WINDOW)
                 nc.vector.tensor_tensor(
                     out=products[:, first_row:SIDE, r, :],
-                    in0=left[b][:, first_row:SIDE, left_r, left_m : left_m + COL_GROUPS, :].rearrange(
+                    in0=left[:, first_row:SIDE, left_r, left_m : left_m + COL_GROUPS, :].rearrange(
                         "p u m t -> p u (m t)"
                     ),
-                    in1=x_right[b][:, first_row + right_shift : SIDE + right_shift, r : r + GRID],
+                    in1=right[:, first_row:SIDE, r : r + GRID],
                     op=mybir.AluOpType.mult,
                 )
+
+        def multiply_below(b, ich, r_order=(0, 1, 2, 3)):
+            below[(b, ich)] = below_pool.tile([P, SIDE, WINDOW, GRID], BF16, name="below", align_bytes=64)
+            multiply(below[(b, ich)], left_below[b], x_below[b], ich, 0, r_order)
+
+        def multiply_above(b, ich):
+            above[(b, ich)] = above_pool.tile([P, SIDE, WINDOW, GRID], BF16, name="above", align_bytes=64)
+            multiply(above[(b, ich)], left_above[b], x_above[b], ich, 1, (0, 1, 2, 3))
+            nc.sync.dma_start(out=lane(above[(LAST, ich)], b + 1, 1, SIDE - 1), in_=lane(above[(b, ich)], 0, 1, SIDE - 1))
+
+        def move_lane(target, source, s, first_row, last_row):
+            nc.sync.dma_start(out=lane(target, s, first_row, last_row), in_=lane(source, s, first_row, last_row))
 
         def contract(b, ich, ir, products):
             codes = code_pool.tile([P, POSITIONS], U32, name="codes", align_bytes=64)
@@ -134,7 +176,8 @@ def tile_fast2order_de_conv_kernel(tc, x, W_words, W_scales, out):
                 scales=scales[:],
                 in_=products[:, ir : ir + GRID].rearrange("p u r k -> p (u r k)"),
             )
-            first = ich == 0 and ir == 0
+            first = b not in opened
+            opened.add(b)
             last = ich == 1 and ir == 2
             a = 2 * ir + ich
             for oh in range(OUT_CH // M_TILE):
@@ -155,46 +198,110 @@ def tile_fast2order_de_conv_kernel(tc, x, W_words, W_scales, out):
                 for oh in range(OUT_CH // M_TILE):
                     for h in range(HALVES):
                         stage = stage_pool.tile([M_TILE, rows, COL_GROUPS, WINDOW], F32, name="stage")
-                        copy = nc.vector.tensor_copy if b == IMAGES - 1 and oh == 1 else nc.scalar.copy
+                        copy = nc.vector.tensor_copy if b == LAST and oh == 1 else nc.scalar.copy
                         copy(
                             out=stage[:],
                             in_=acc[(b, oh, h)][:].rearrange("p (y r m) -> p y m r", r=WINDOW, m=COL_GROUPS),
                         )
-                        nc.sync.dma_start(
+                        store_queue = nc.sync if b == LAST else nc.scalar
+                        store_queue.dma_start(
                             out=out[b, M_TILE * oh : M_TILE * (oh + 1), rows * h : rows * (h + 1), :].rearrange(
                                 "o y z -> o (y z)"
                             ),
                             in_=stage[:].rearrange("p y m r -> p (y m r)"),
                         )
 
-        groups = [(b, ich) for b in range(IMAGES) for ich in range(2)]
-        for k in range(len(groups) + 1):
-            new = groups[k] if k < len(groups) else None
-            old = groups[k - 1] if k > 0 else None
-            if new is not None:
-                b, ich = new
-                if b + 1 < IMAGES:
-                    for r in range(WINDOW):
-                        if ich == 0:
-                            expand_left(nc.scalar.copy, b + 1, r)
-                below[new] = prod_pool.tile([P, SIDE, WINDOW, GRID], BF16, name="below", align_bytes=64)
-                multiply(below[new], b, ich, 0, WINDOW)
-            if old is not None:
-                contract(old[0], old[1], 3, above[old])
-                nc.sync.dma_start(out=lane(above[old], 1, 2, GRID + 1), in_=lane(below[old], 1, 2, GRID + 1))
-            if new is not None:
-                above[new] = prod_pool.tile([P, SIDE, WINDOW, GRID], BF16, name="above", align_bytes=64)
-                multiply(above[new], new[0], new[1], 1, 0)
-                nc.sync.dma_start(out=lane(above[new], 0, 2, SIDE - 1), in_=lane(below[new], 0, 2, SIDE - 1))
-            if old is not None:
-                contract(old[0], old[1], 1, below[old])
-            if new is not None:
-                contract(new[0], new[1], 0, below[new])
-                nc.sync.dma_start(out=lane(below[new], 3, 1, GRID), in_=lane(above[new], 3, 1, GRID))
-                if k == 0:
-                    for ir in (0, 3, 1, 2):
-                        load_weights(1, ir)
-                if new[1] == 0 and new[0] + 2 < IMAGES:
-                    load_x(new[0] + 2)
-            if old is not None:
-                contract(old[0], old[1], 2, above[old])
+        def pass_0(b, ich):
+            contract(b, ich, 0, below[(b, ich)])
+
+        def after_pass_0(b, ich):
+            move_lane(below[(b, ich)], above[(b, ich)], 3, 1, GRID)
+
+        def pass_1(b, ich):
+            contract(b, ich, 1, below[(b, ich)])
+
+        def before_pass_3(b, ich):
+            move_lane(above[(b, ich)], below[(b, ich)], 0, 2, SIDE - 1)
+
+        def pass_3(b, ich):
+            contract(b, ich, 3, above[(b, ich)])
+            move_lane(above[(b, ich)], below[(b, ich)], 1, 2, GRID + 1)
+
+        def pass_2(b, ich):
+            contract(b, ich, 2, above[(b, ich)])
+
+        for ich in range(2):
+            above[(LAST, ich)] = keep.tile([P, SIDE, WINDOW, GRID], BF16, name="above_last%d" % ich, align_bytes=64)
+
+        load_x(0)
+        left_below[0] = new_left("left_below")
+        for r in range(WINDOW):
+            copy = nc.scalar.copy if r < 2 else nc.vector.tensor_copy
+            expand_left(copy, left_below[0], x_left[0], r, 0)
+        for s in range(WINDOW):
+            load_left_lane(x_left_above0, 0 if s > 0 else LAST, s)
+        load_x_above(0)
+        expand_above(0, x_left_above0)
+        scale_rows = W_scales.rearrange("g q n -> (g q) n").rearrange("(c a) n -> c (a n)", a=PASSES).bitcast(I32)
+        for quadrant in range(4):
+            nc.sync.dma_start(
+                out=w_scales[32 * quadrant : 32 * quadrant + 4].rearrange("p a n -> p (a n)").bitcast(I32),
+                in_=scale_rows[4 * quadrant : 4 * quadrant + 4, :],
+            )
+        load_weights(0, 0)
+        load_weights(1, 0)
+        load_x(1)
+        load_weights(0, 1)
+        load_weights(0, 3)
+        expand_below(1)
+        multiply_below(0, 0, (2, 3, 0, 1))
+        multiply_below(0, 1)
+        pass_0(0, 0)
+        pass_0(0, 1)
+        multiply_above(0, 0)
+        after_pass_0(0, 0)
+        before_pass_3(0, 0)
+        multiply_above(0, 1)
+        after_pass_0(0, 1)
+        before_pass_3(0, 1)
+        prepare_above(1)
+        load_weights(1, 1)
+        load_weights(1, 3)
+
+        for b in range(1, IMAGES):
+            if b < LAST:
+                expand_above(b, x_left[b])
+            for ich in range(2):
+                multiply_below(b, ich)
+                if b == LAST:
+                    before_pass_3(b, ich)
+                pass_1(b - 1, ich)
+                pass_3(b - 1, ich)
+                if ich == 0:
+                    if b == 1:
+                        load_weights(0, 2)
+                        load_weights(1, 2)
+                    if b < LAST:
+                        load_x(b + 1)
+                        expand_below(b + 1)
+            if b < LAST:
+                for ich in range(2):
+                    multiply_above(b, ich)
+                    pass_2(b - 1, ich)
+                    pass_0(b, ich)
+                    after_pass_0(b, ich)
+                    before_pass_3(b, ich)
+                if b + 1 < LAST:
+                    prepare_above(b + 1)
+        pass_2(LAST - 1, 0)
+        pass_0(LAST, 0)
+        after_pass_0(LAST, 0)
+        pass_0(LAST, 1)
+        after_pass_0(LAST, 1)
+        pass_2(LAST - 1, 1)
+        pass_3(LAST, 0)
+        pass_3(LAST, 1)
+        pass_1(LAST, 0)
+        pass_1(LAST, 1)
+        pass_2(LAST, 0)
+        pass_2(LAST, 1)

@@ -19,8 +19,11 @@ SIDE = 35
 PIXELS = SIDE * SIDE
 GRID = 32
 WINDOW = 4
-COL_GROUPS = GRID // WINDOW
-LEFT_GROUPS = 12
+LEFT_PAIRS = 17
+PAIR_RUNS = ((0, 16, 0, 17), (-1, 36, 1, 16), (1, 0, 0, 16))
+SLOTS = 56
+SPLIT_ROW = 20
+JOIN_SLOTS = ((16, 20), (0, 17))
 OUT_CH = 256
 M_TILE = 128
 N_TILE = 512
@@ -35,9 +38,10 @@ def tile_fast2order_de_conv_kernel(tc, x, W_words, W_scales, out):
     with ExitStack() as ctx:
         ctx.enter_context(tc.manual_schedule())
         keep = ctx.enter_context(tc.tile_pool(name="keep", bufs=1))
-        left_pool = ctx.enter_context(tc.tile_pool(name="left", bufs=2))
+        doubled_pool = ctx.enter_context(tc.tile_pool(name="doubled", bufs=2))
+        pair_pool = ctx.enter_context(tc.tile_pool(name="pairs", bufs=1))
         below_pool = ctx.enter_context(tc.tile_pool(name="below", bufs=4))
-        above_pool = ctx.enter_context(tc.tile_pool(name="above", bufs=3))
+        above_pool = ctx.enter_context(tc.tile_pool(name="above", bufs=4))
         code_pool = ctx.enter_context(tc.tile_pool(name="code", bufs=4))
         stage_pool = ctx.enter_context(tc.tile_pool(name="stage", bufs=4))
         psum = ctx.enter_context(tc.psum_pool(name="acc", bufs=2))
@@ -111,30 +115,28 @@ def tile_fast2order_de_conv_kernel(tc, x, W_words, W_scales, out):
                         out=w_words[s:P:WINDOW, a, :].bitcast(I32), in_=word_rows[a, (s + ir) % WINDOW]
                     )
 
-        def expand_left(copy, tile, source, r, first_row):
-            groups_here = COL_GROUPS + 1 if r < 2 else COL_GROUPS
-            rows = source[:].rearrange("p (h w) -> p h w", w=SIDE)
-            picked = rows[:, first_row:SIDE, r : r + WINDOW * (groups_here - 1) + 1 : WINDOW]
+        doubled_below = {}
+        doubled_above = {}
+
+        def new_doubled(name):
+            return doubled_pool.tile([P, SIDE, 2, LEFT_PAIRS, 2], BF16, name=name)
+
+        def double_left(copy, tile, source, first_row, last_row):
+            rows = source[:].rearrange("p (u w) -> p u w", w=SIDE)[:, first_row : last_row + 1, 0 : 2 * LEFT_PAIRS]
             copy(
-                out=tile[:, first_row:SIDE, r, 0:groups_here, :],
-                in_=picked.unsqueeze(3).to_broadcast([P, SIDE - first_row, groups_here, WINDOW]),
+                out=tile[:, first_row : last_row + 1],
+                in_=rows.rearrange("p u (q h) -> p u h q", h=2)
+                .unsqueeze(4)
+                .to_broadcast([P, last_row + 1 - first_row, 2, LEFT_PAIRS, 2]),
             )
 
-        left_below = {}
-        left_above = {}
+        def double_below(copy, b):
+            doubled_below[b] = new_doubled("doubled_below")
+            double_left(copy, doubled_below[b], x_left[b], 0, SIDE - 1)
 
-        def new_left(name):
-            return left_pool.tile([P, SIDE, WINDOW, LEFT_GROUPS, WINDOW], BF16, name=name)
-
-        def expand_below(b):
-            left_below[b] = new_left("left_below")
-            for r in range(WINDOW):
-                expand_left(nc.scalar.copy, left_below[b], x_left[b], r, 0)
-
-        def expand_above(b, source):
-            left_above[b] = new_left("left_above")
-            for r in range(WINDOW):
-                expand_left(nc.scalar.copy, left_above[b], source, r, 1)
+        def double_above(copy, b, source):
+            doubled_above[b] = new_doubled("doubled_above")
+            double_left(copy, doubled_above[b], source, 1, SIDE - 1)
 
         below = {}
         above = {}
@@ -144,25 +146,55 @@ def tile_fast2order_de_conv_kernel(tc, x, W_words, W_scales, out):
         def lane(products, s, first_row, last_row):
             return products[s:P:WINDOW, first_row : last_row + 1]
 
-        def multiply(products, left, right, ich, first_row, r_order):
-            for r in r_order:
-                left_m, left_r = divmod(r + 2 * ich, WINDOW)
-                nc.vector.tensor_tensor(
-                    out=products[:, first_row:SIDE, r, :],
-                    in0=left[:, first_row:SIDE, left_r, left_m : left_m + COL_GROUPS, :].rearrange(
-                        "p u m t -> p u (m t)"
-                    ),
-                    in1=right[:, first_row:SIDE, r : r + GRID],
-                    op=mybir.AluOpType.mult,
-                )
+        def multiply(pairs, doubled, right, first_row, runs=PAIR_RUNS):
+            for j, slot, first_q, count in runs:
+                for h in range(2):
+                    nc.vector.tensor_tensor(
+                        out=pairs[:, first_row:SIDE, h, slot : slot + count, :].rearrange("p u q e -> p u (q e)"),
+                        in0=doubled[:, first_row:SIDE, h, first_q + j : first_q + j + count, :].rearrange(
+                            "p u q e -> p u (q e)"
+                        ),
+                        in1=right[:, first_row:SIDE, h + 2 * first_q : h + 2 * (first_q + count)],
+                        op=mybir.AluOpType.mult,
+                    )
 
-        def multiply_below(b, ich, r_order=(0, 1, 2, 3)):
-            below[(b, ich)] = below_pool.tile([P, SIDE, WINDOW, GRID], BF16, name="below", align_bytes=64)
-            multiply(below[(b, ich)], left_below[b], x_below[b], ich, 0, r_order)
+        def join(products, pairs, ich, first_row):
+            slot, distance = JOIN_SLOTS[ich]
+            halves = (
+                pairs[:, first_row:SIDE, :, slot : slot + 2 * distance, :]
+                .rearrange("p u h s e -> p (u h) (s e)")
+                .bitcast(F32)
+                .rearrange("p a (f s) -> p a s f", f=2)
+            )
+            nc.scalar.copy(
+                out=products[:, first_row:SIDE]
+                .rearrange("p u h k -> p (u h k)")
+                .bitcast(F32)
+                .rearrange("p (a q f) -> p a q f", q=GRID // 2, f=2),
+                in_=halves[:, :, 0 : GRID // 2, :],
+            )
 
-        def multiply_above(b, ich):
-            above[(b, ich)] = above_pool.tile([P, SIDE, WINDOW, GRID], BF16, name="above", align_bytes=64)
-            multiply(above[(b, ich)], left_above[b], x_above[b], ich, 1, (0, 1, 2, 3))
+        pairs_below = {}
+        pairs_above = {}
+
+        def multiply_below(b, runs=PAIR_RUNS):
+            if b not in pairs_below:
+                pairs_below[b] = pair_pool.tile([P, SIDE, 2, SLOTS, 2], BF16, name="pairs_below", align_bytes=64)
+            multiply(pairs_below[b], doubled_below[b], x_below[b], 0, runs)
+
+        def multiply_above(b):
+            pairs_above[b] = pair_pool.tile([P, SIDE, 2, SLOTS, 2], BF16, name="pairs_above", align_bytes=64)
+            multiply(pairs_above[b], doubled_above[b], x_above[b], 1)
+
+        def join_below(b, ich):
+            below[(b, ich)] = below_pool.tile([P, SIDE, 2, 2 * GRID], BF16, name="below", align_bytes=64)
+            join(below[(b, ich)], pairs_below[b], ich, 0)
+
+        def join_above(b, ich):
+            above[(b, ich)] = above_pool.tile([P, SIDE, 2, 2 * GRID], BF16, name="above", align_bytes=64)
+            join(above[(b, ich)], pairs_above[b], ich, 1)
+
+        def park(b, ich):
             nc.sync.dma_start(out=lane(above[(LAST, ich)], b + 1, 1, SIDE - 1), in_=lane(above[(b, ich)], 0, 1, SIDE - 1))
 
         def move_lane(target, source, s, first_row, last_row):
@@ -171,17 +203,24 @@ def tile_fast2order_de_conv_kernel(tc, x, W_words, W_scales, out):
         def contract(b, ich, ir, products):
             codes = code_pool.tile([P, POSITIONS], U32, name="codes", align_bytes=64)
             scales = code_pool.tile([P, POSITIONS], U8, name="scales", align_bytes=64)
+            last = ich == 1 and ir == 2
+            parts = [[0], [1]] if last and b == LAST else [[0, 1]]
+            for part in parts:
+                contract_halves(b, ich, ir, products, codes, scales, part, last)
+
+        def contract_halves(b, ich, ir, products, codes, scales, part, last):
+            rows = GRID // HALVES
+            columns = slice(N_TILE * part[0], N_TILE * (part[-1] + 1))
             nc.vector.quantize_mx(
-                out=codes[:].bitcast(FP8X4),
-                scales=scales[:],
-                in_=products[:, ir : ir + GRID].rearrange("p u r k -> p (u r k)"),
+                out=codes[:, columns].bitcast(FP8X4),
+                scales=scales[:, columns],
+                in_=products[:, ir + rows * part[0] : ir + rows * (part[-1] + 1)].rearrange("p u h k -> p (u h k)"),
             )
             first = b not in opened
             opened.add(b)
-            last = ich == 1 and ir == 2
             a = 2 * ir + ich
             for oh in range(OUT_CH // M_TILE):
-                for h in range(HALVES):
+                for h in part:
                     if first:
                         acc[(b, oh, h)] = psum.tile([M_TILE, N_TILE], F32, name="acc%d%d" % (oh, h))
                     nc.tensor.matmul_mx(
@@ -194,21 +233,20 @@ def tile_fast2order_de_conv_kernel(tc, x, W_words, W_scales, out):
                         stop=last,
                     )
             if last:
-                rows = GRID // HALVES
                 for oh in range(OUT_CH // M_TILE):
-                    for h in range(HALVES):
-                        stage = stage_pool.tile([M_TILE, rows, COL_GROUPS, WINDOW], F32, name="stage")
-                        copy = nc.vector.tensor_copy if b == LAST and oh == 1 else nc.scalar.copy
+                    for h in part:
+                        stage = stage_pool.tile([M_TILE, rows, GRID // 2, 2], F32, name="stage")
+                        copy = nc.vector.tensor_copy if b == LAST and oh == 0 and h == 1 else nc.scalar.copy
                         copy(
                             out=stage[:],
-                            in_=acc[(b, oh, h)][:].rearrange("p (y r m) -> p y m r", r=WINDOW, m=COL_GROUPS),
+                            in_=acc[(b, oh, h)][:].rearrange("p (y h q) -> p y q h", h=2, q=GRID // 2),
                         )
                         store_queue = nc.sync if b == LAST else nc.scalar
                         store_queue.dma_start(
                             out=out[b, M_TILE * oh : M_TILE * (oh + 1), rows * h : rows * (h + 1), :].rearrange(
                                 "o y z -> o (y z)"
                             ),
-                            in_=stage[:].rearrange("p y m r -> p (y m r)"),
+                            in_=stage[:].rearrange("p y q h -> p (y q h)"),
                         )
 
         def pass_0(b, ich):
@@ -231,17 +269,15 @@ def tile_fast2order_de_conv_kernel(tc, x, W_words, W_scales, out):
             contract(b, ich, 2, above[(b, ich)])
 
         for ich in range(2):
-            above[(LAST, ich)] = keep.tile([P, SIDE, WINDOW, GRID], BF16, name="above_last%d" % ich, align_bytes=64)
+            above[(LAST, ich)] = keep.tile([P, SIDE, 2, 2 * GRID], BF16, name="above_last%d" % ich, align_bytes=64)
 
         load_x(0)
-        left_below[0] = new_left("left_below")
-        for r in range(WINDOW):
-            copy = nc.scalar.copy if r < 2 else nc.vector.tensor_copy
-            expand_left(copy, left_below[0], x_left[0], r, 0)
+        doubled_below[0] = new_doubled("doubled_below")
+        double_left(nc.vector.tensor_copy, doubled_below[0], x_left[0], 0, SPLIT_ROW - 1)
+        double_left(nc.scalar.copy, doubled_below[0], x_left[0], SPLIT_ROW, SIDE - 1)
         for s in range(WINDOW):
             load_left_lane(x_left_above0, 0 if s > 0 else LAST, s)
         load_x_above(0)
-        expand_above(0, x_left_above0)
         scale_rows = W_scales.rearrange("g q n -> (g q) n").rearrange("(c a) n -> c (a n)", a=PASSES).bitcast(I32)
         for quadrant in range(4):
             nc.sync.dma_start(
@@ -253,55 +289,96 @@ def tile_fast2order_de_conv_kernel(tc, x, W_words, W_scales, out):
         load_x(1)
         load_weights(0, 1)
         load_weights(0, 3)
-        expand_below(1)
-        multiply_below(0, 0, (2, 3, 0, 1))
-        multiply_below(0, 1)
-        pass_0(0, 0)
-        pass_0(0, 1)
-        multiply_above(0, 0)
-        after_pass_0(0, 0)
-        before_pass_3(0, 0)
-        multiply_above(0, 1)
-        after_pass_0(0, 1)
-        before_pass_3(0, 1)
+        multiply_below(0)
+        join_below(0, 0)
+        join_below(0, 1)
+        double_above(nc.vector.tensor_copy, 0, x_left_above0)
+        multiply_above(0)
+        double_below(nc.scalar.copy, 1)
         prepare_above(1)
         load_weights(1, 1)
         load_weights(1, 3)
+        pass_0(0, 0)
+        pass_0(0, 1)
+        join_above(0, 0)
+        park(0, 0)
+        after_pass_0(0, 0)
+        join_above(0, 1)
+        park(0, 1)
+        after_pass_0(0, 1)
+        before_pass_3(0, 0)
+        before_pass_3(0, 1)
+        load_x(2)
 
-        for b in range(1, IMAGES):
-            if b < LAST:
-                expand_above(b, x_left[b])
-            for ich in range(2):
-                multiply_below(b, ich)
-                if b == LAST:
-                    before_pass_3(b, ich)
-                pass_1(b - 1, ich)
-                pass_3(b - 1, ich)
-                if ich == 0:
-                    if b == 1:
-                        load_weights(0, 2)
-                        load_weights(1, 2)
-                    if b < LAST:
-                        load_x(b + 1)
-                        expand_below(b + 1)
-            if b < LAST:
-                for ich in range(2):
-                    multiply_above(b, ich)
-                    pass_2(b - 1, ich)
-                    pass_0(b, ich)
-                    after_pass_0(b, ich)
-                    before_pass_3(b, ich)
-                if b + 1 < LAST:
-                    prepare_above(b + 1)
-        pass_2(LAST - 1, 0)
-        pass_0(LAST, 0)
-        after_pass_0(LAST, 0)
-        pass_0(LAST, 1)
-        after_pass_0(LAST, 1)
-        pass_2(LAST - 1, 1)
-        pass_3(LAST, 0)
-        pass_3(LAST, 1)
-        pass_1(LAST, 0)
-        pass_1(LAST, 1)
-        pass_2(LAST, 0)
-        pass_2(LAST, 1)
+        multiply_below(1)
+        join_below(1, 0)
+        join_below(1, 1)
+        double_above(nc.vector.tensor_copy, 1, x_left[1])
+        pass_1(0, 0)
+        multiply_above(1)
+        pass_3(0, 0)
+        load_weights(0, 2)
+        load_weights(1, 2)
+        join_above(1, 0)
+        park(1, 0)
+        pass_1(0, 1)
+        pass_3(0, 1)
+        join_above(1, 1)
+        park(1, 1)
+        pass_0(1, 0)
+        after_pass_0(1, 0)
+        before_pass_3(1, 0)
+        pass_2(0, 0)
+        double_below(nc.scalar.copy, 2)
+        pass_0(1, 1)
+        after_pass_0(1, 1)
+        before_pass_3(1, 1)
+        prepare_above(2)
+        double_above(nc.scalar.copy, 2, x_left[2])
+        load_x(3)
+        pass_2(0, 1)
+
+        multiply_below(2)
+        join_below(2, 0)
+        join_below(2, 1)
+        pass_1(1, 0)
+        pass_3(1, 0)
+        multiply_above(2)
+        double_below(nc.scalar.copy, 3)
+        join_above(2, 0)
+        pass_1(1, 1)
+        pass_3(1, 1)
+        join_above(2, 1)
+        pass_0(2, 0)
+        pass_2(1, 0)
+        park(2, 0)
+        after_pass_0(2, 0)
+        pass_0(2, 1)
+        park(2, 1)
+        after_pass_0(2, 1)
+        before_pass_3(2, 0)
+        before_pass_3(2, 1)
+        pass_2(1, 1)
+
+        multiply_below(3, PAIR_RUNS[:2])
+        join_below(3, 0)
+        pass_1(2, 0)
+        pass_3(2, 0)
+        before_pass_3(3, 0)
+        pass_1(2, 1)
+        pass_3(2, 1)
+        multiply_below(3, PAIR_RUNS[2:])
+        join_below(3, 1)
+        pass_0(3, 0)
+        after_pass_0(3, 0)
+        pass_2(2, 0)
+        before_pass_3(3, 1)
+        pass_2(2, 1)
+        pass_0(3, 1)
+        after_pass_0(3, 1)
+        pass_3(3, 0)
+        pass_3(3, 1)
+        pass_1(3, 0)
+        pass_1(3, 1)
+        pass_2(3, 0)
+        pass_2(3, 1)

@@ -81,11 +81,17 @@ def tile_fast2order_de_conv_kernel(tc, x, W_words, W_scales, out):
                 .to_broadcast([CHANNELS, 2, count * SIDE]),
             )
 
-        def load_x(b):
+        def load_left(b):
             for s in range(WINDOW):
                 load_left_lane(x_left[b], b, s)
+
+        def load_below(b):
             for s in range(WINDOW):
                 load_rows(x_below[b], b, s, s, 0, SIDE - s)
+
+        def load_x(b):
+            load_left(b)
+            load_below(b)
 
         def load_x_above(b):
             for s in range(WINDOW):
@@ -115,6 +121,9 @@ def tile_fast2order_de_conv_kernel(tc, x, W_words, W_scales, out):
                         out=w_words[s:P:WINDOW, a, :].bitcast(I32), in_=word_rows[a, (s + ir) % WINDOW]
                     )
 
+        def lane(tile, s, first_row, last_row):
+            return tile[s:P:WINDOW, first_row : last_row + 1]
+
         doubled_below = {}
         doubled_above = {}
 
@@ -134,6 +143,12 @@ def tile_fast2order_de_conv_kernel(tc, x, W_words, W_scales, out):
             doubled_below[b] = new_doubled("doubled_below")
             double_left(copy, doubled_below[b], x_left[b], 0, SIDE - 1)
 
+        def turn_above(b):
+            nc.sync.dma_start(
+                out=lane(doubled_below[b], 0, 1, SIDE - 1), in_=lane(doubled_below[LAST], 0, 1, SIDE - 1)
+            )
+            doubled_above[b] = doubled_below[b]
+
         def double_above(copy, b, source):
             doubled_above[b] = new_doubled("doubled_above")
             double_left(copy, doubled_above[b], source, 1, SIDE - 1)
@@ -142,9 +157,6 @@ def tile_fast2order_de_conv_kernel(tc, x, W_words, W_scales, out):
         above = {}
         acc = {}
         opened = set()
-
-        def lane(products, s, first_row, last_row):
-            return products[s:P:WINDOW, first_row : last_row + 1]
 
         def multiply(pairs, doubled, right, first_row, runs=PAIR_RUNS):
             for j, slot, first_q, count in runs:
@@ -296,8 +308,6 @@ def tile_fast2order_de_conv_kernel(tc, x, W_words, W_scales, out):
         multiply_above(0)
         double_below(nc.scalar.copy, 1)
         prepare_above(1)
-        load_weights(1, 1)
-        load_weights(1, 3)
         pass_0(0, 0)
         pass_0(0, 1)
         join_above(0, 0)
@@ -306,8 +316,10 @@ def tile_fast2order_de_conv_kernel(tc, x, W_words, W_scales, out):
         join_above(0, 1)
         park(0, 1)
         after_pass_0(0, 1)
+        load_weights(1, 1)
         before_pass_3(0, 0)
         before_pass_3(0, 1)
+        load_weights(1, 3)
         load_x(2)
 
         multiply_below(1)
@@ -317,42 +329,43 @@ def tile_fast2order_de_conv_kernel(tc, x, W_words, W_scales, out):
         pass_1(0, 0)
         multiply_above(1)
         pass_3(0, 0)
-        load_weights(0, 2)
-        load_weights(1, 2)
+        load_left(3)
         join_above(1, 0)
         park(1, 0)
+        load_weights(0, 2)
         pass_1(0, 1)
         pass_3(0, 1)
+        load_weights(1, 2)
         join_above(1, 1)
         park(1, 1)
         pass_0(1, 0)
         after_pass_0(1, 0)
         before_pass_3(1, 0)
-        pass_2(0, 0)
         double_below(nc.scalar.copy, 2)
+        double_below(nc.scalar.copy, 3)
         pass_0(1, 1)
+        pass_2(0, 0)
         after_pass_0(1, 1)
         before_pass_3(1, 1)
-        prepare_above(2)
-        double_above(nc.scalar.copy, 2, x_left[2])
-        load_x(3)
+        load_x_above(2)
+        load_below(3)
         pass_2(0, 1)
 
         multiply_below(2)
+        turn_above(2)
         join_below(2, 0)
         join_below(2, 1)
         pass_1(1, 0)
         pass_3(1, 0)
-        multiply_above(2)
-        double_below(nc.scalar.copy, 3)
-        join_above(2, 0)
         pass_1(1, 1)
+        multiply_above(2)
+        join_above(2, 0)
         pass_3(1, 1)
         join_above(2, 1)
         pass_0(2, 0)
-        pass_2(1, 0)
         park(2, 0)
         after_pass_0(2, 0)
+        pass_2(1, 0)
         pass_0(2, 1)
         park(2, 1)
         after_pass_0(2, 1)

@@ -22,6 +22,7 @@ WINDOW = 4
 LEFT_PAIRS = 17
 PAIR_RUNS = ((0, 16, 0, 17), (-1, 36, 1, 16), (1, 0, 0, 16))
 SLOTS = 56
+GAPS = ((33, 3), (52, 4))
 SPLIT_ROW = 20
 JOIN_SLOTS = ((16, 20), (0, 17))
 OUT_CH = 256
@@ -124,6 +125,11 @@ def tile_fast2order_de_conv_kernel(tc, x, W_words, W_scales, out):
         def lane(tile, s, first_row, last_row):
             return tile[s:P:WINDOW, first_row : last_row + 1]
 
+        def move_lane(target, to, source, s, first_row, last_row):
+            nc.sync.dma_start(
+                out=lane(target, to, first_row, last_row), in_=lane(source, s, first_row, last_row)
+            )
+
         doubled_below = {}
         doubled_above = {}
 
@@ -144,9 +150,7 @@ def tile_fast2order_de_conv_kernel(tc, x, W_words, W_scales, out):
             double_left(copy, doubled_below[b], x_left[b], 0, SIDE - 1)
 
         def turn_above(b):
-            nc.sync.dma_start(
-                out=lane(doubled_below[b], 0, 1, SIDE - 1), in_=lane(doubled_below[LAST], 0, 1, SIDE - 1)
-            )
+            move_lane(doubled_below[b], 0, doubled_below[LAST], 0, 1, SIDE - 1)
             doubled_above[b] = doubled_below[b]
 
         def double_above(copy, b, source):
@@ -188,6 +192,10 @@ def tile_fast2order_de_conv_kernel(tc, x, W_words, W_scales, out):
 
         pairs_below = {}
         pairs_above = {}
+        pairs_shared = keep.tile([P, SIDE, 2, SLOTS, 2], BF16, name="pairs_shared", align_bytes=64)
+        pairs_last = keep.tile([P, SIDE, 2, SLOTS, 2], BF16, name="pairs_last", align_bytes=64)
+        for slot, count in GAPS:
+            nc.vector.memset(pairs_shared[:, :, :, slot : slot + count, :], 0)
 
         def multiply_below(b, runs=PAIR_RUNS):
             if b not in pairs_below:
@@ -195,8 +203,12 @@ def tile_fast2order_de_conv_kernel(tc, x, W_words, W_scales, out):
             multiply(pairs_below[b], doubled_below[b], x_below[b], 0, runs)
 
         def multiply_above(b):
-            pairs_above[b] = pair_pool.tile([P, SIDE, 2, SLOTS, 2], BF16, name="pairs_above", align_bytes=64)
+            pairs_above[b] = pairs_shared
             multiply(pairs_above[b], doubled_above[b], x_above[b], 1)
+            move_lane(pairs_last, b + 1, pairs_shared, 0, 1, SIDE - 1)
+            if b + 1 == LAST:
+                move_lane(pairs_last, 0, pairs_shared, 0, 1, SIDE - 1)
+                pairs_above[LAST] = pairs_last
 
         def join_below(b, ich):
             below[(b, ich)] = below_pool.tile([P, SIDE, 2, 2 * GRID], BF16, name="below", align_bytes=64)
@@ -205,12 +217,6 @@ def tile_fast2order_de_conv_kernel(tc, x, W_words, W_scales, out):
         def join_above(b, ich):
             above[(b, ich)] = above_pool.tile([P, SIDE, 2, 2 * GRID], BF16, name="above", align_bytes=64)
             join(above[(b, ich)], pairs_above[b], ich, 1)
-
-        def park(b, ich):
-            nc.sync.dma_start(out=lane(above[(LAST, ich)], b + 1, 1, SIDE - 1), in_=lane(above[(b, ich)], 0, 1, SIDE - 1))
-
-        def move_lane(target, source, s, first_row, last_row):
-            nc.sync.dma_start(out=lane(target, s, first_row, last_row), in_=lane(source, s, first_row, last_row))
 
         def contract(b, ich, ir, products):
             codes = code_pool.tile([P, POSITIONS], U32, name="codes", align_bytes=64)
@@ -244,44 +250,56 @@ def tile_fast2order_de_conv_kernel(tc, x, W_words, W_scales, out):
                         start=first,
                         stop=last,
                     )
-            if last:
+            if last and b == LAST:
                 for oh in range(OUT_CH // M_TILE):
                     for h in part:
-                        stage = stage_pool.tile([M_TILE, rows, GRID // 2, 2], F32, name="stage")
-                        copy = nc.vector.tensor_copy if b == LAST and oh == 0 and h == 1 else nc.scalar.copy
-                        copy(
-                            out=stage[:],
-                            in_=acc[(b, oh, h)][:].rearrange("p (y h q) -> p y q h", h=2, q=GRID // 2),
-                        )
-                        store_queue = nc.sync if b == LAST else nc.scalar
-                        store_queue.dma_start(
-                            out=out[b, M_TILE * oh : M_TILE * (oh + 1), rows * h : rows * (h + 1), :].rearrange(
-                                "o y z -> o (y z)"
-                            ),
-                            in_=stage[:].rearrange("p y q h -> p (y q h)"),
-                        )
+                        empty_bank(nc.vector.tensor_copy if oh == 0 and h == 1 else nc.scalar.copy, b, oh, h)
+                        store_bank(b, oh, h)
+
+        staged = {}
+
+        def empty_bank(copy, b, oh, h):
+            stage = stage_pool.tile([M_TILE, GRID // HALVES, GRID // 2, 2], F32, name="stage")
+            copy(out=stage[:], in_=acc[(b, oh, h)][:].rearrange("p (y h q) -> p y q h", h=2, q=GRID // 2))
+            staged[(b, oh, h)] = stage
+
+        def store_bank(b, oh, h):
+            rows = GRID // HALVES
+            nc.sync.dma_start(
+                out=out[b, M_TILE * oh : M_TILE * (oh + 1), rows * h : rows * (h + 1), :].rearrange(
+                    "o y z -> o (y z)"
+                ),
+                in_=staged[(b, oh, h)][:].rearrange("p y q h -> p (y q h)"),
+            )
+
+        def empty(b):
+            for oh in range(OUT_CH // M_TILE):
+                for h in range(HALVES):
+                    empty_bank(nc.scalar.copy, b, oh, h)
+
+        def store(b):
+            for oh in range(OUT_CH // M_TILE):
+                for h in range(HALVES):
+                    store_bank(b, oh, h)
 
         def pass_0(b, ich):
             contract(b, ich, 0, below[(b, ich)])
 
         def after_pass_0(b, ich):
-            move_lane(below[(b, ich)], above[(b, ich)], 3, 1, GRID)
+            move_lane(below[(b, ich)], 3, above[(b, ich)], 3, 1, GRID)
 
         def pass_1(b, ich):
             contract(b, ich, 1, below[(b, ich)])
 
         def before_pass_3(b, ich):
-            move_lane(above[(b, ich)], below[(b, ich)], 0, 2, SIDE - 1)
+            move_lane(above[(b, ich)], 0, below[(b, ich)], 0, 2, SIDE - 1)
 
         def pass_3(b, ich):
             contract(b, ich, 3, above[(b, ich)])
-            move_lane(above[(b, ich)], below[(b, ich)], 1, 2, GRID + 1)
+            move_lane(above[(b, ich)], 1, below[(b, ich)], 1, 2, GRID + 1)
 
         def pass_2(b, ich):
             contract(b, ich, 2, above[(b, ich)])
-
-        for ich in range(2):
-            above[(LAST, ich)] = keep.tile([P, SIDE, 2, 2 * GRID], BF16, name="above_last%d" % ich, align_bytes=64)
 
         load_x(0)
         doubled_below[0] = new_doubled("doubled_below")
@@ -309,16 +327,14 @@ def tile_fast2order_de_conv_kernel(tc, x, W_words, W_scales, out):
         double_below(nc.scalar.copy, 1)
         prepare_above(1)
         pass_0(0, 0)
-        pass_0(0, 1)
         join_above(0, 0)
-        park(0, 0)
         after_pass_0(0, 0)
-        join_above(0, 1)
-        park(0, 1)
-        after_pass_0(0, 1)
-        load_weights(1, 1)
         before_pass_3(0, 0)
+        pass_0(0, 1)
+        join_above(0, 1)
+        after_pass_0(0, 1)
         before_pass_3(0, 1)
+        load_weights(1, 1)
         load_weights(1, 3)
         load_x(2)
 
@@ -327,70 +343,73 @@ def tile_fast2order_de_conv_kernel(tc, x, W_words, W_scales, out):
         join_below(1, 1)
         double_above(nc.vector.tensor_copy, 1, x_left[1])
         pass_1(0, 0)
-        multiply_above(1)
         pass_3(0, 0)
-        load_left(3)
-        join_above(1, 0)
-        park(1, 0)
         load_weights(0, 2)
+        load_left(3)
+        multiply_above(1)
+        join_above(1, 0)
+        before_pass_3(1, 0)
         pass_1(0, 1)
         pass_3(0, 1)
-        load_weights(1, 2)
         join_above(1, 1)
-        park(1, 1)
+        load_weights(1, 2)
         pass_0(1, 0)
         after_pass_0(1, 0)
-        before_pass_3(1, 0)
         double_below(nc.scalar.copy, 2)
-        double_below(nc.scalar.copy, 3)
         pass_0(1, 1)
-        pass_2(0, 0)
-        after_pass_0(1, 1)
         before_pass_3(1, 1)
+        after_pass_0(1, 1)
         load_x_above(2)
-        load_below(3)
+        pass_2(0, 0)
+        double_below(nc.scalar.copy, 3)
         pass_2(0, 1)
+        empty(0)
 
         multiply_below(2)
         turn_above(2)
+        load_below(3)
         join_below(2, 0)
         join_below(2, 1)
         pass_1(1, 0)
         pass_3(1, 0)
         pass_1(1, 1)
+        store(0)
         multiply_above(2)
         join_above(2, 0)
+        before_pass_3(2, 0)
         pass_3(1, 1)
         join_above(2, 1)
         pass_0(2, 0)
-        park(2, 0)
         after_pass_0(2, 0)
-        pass_2(1, 0)
-        pass_0(2, 1)
-        park(2, 1)
-        after_pass_0(2, 1)
-        before_pass_3(2, 0)
         before_pass_3(2, 1)
+        pass_0(2, 1)
+        after_pass_0(2, 1)
+        pass_2(1, 0)
         pass_2(1, 1)
 
-        multiply_below(3, PAIR_RUNS[:2])
+        multiply_below(3)
+        join_above(3, 0)
         join_below(3, 0)
+        join_above(3, 1)
+        before_pass_3(3, 0)
+        join_below(3, 1)
+        empty(1)
         pass_1(2, 0)
         pass_3(2, 0)
-        before_pass_3(3, 0)
+        before_pass_3(3, 1)
         pass_1(2, 1)
         pass_3(2, 1)
-        multiply_below(3, PAIR_RUNS[2:])
-        join_below(3, 1)
         pass_0(3, 0)
         after_pass_0(3, 0)
         pass_2(2, 0)
-        before_pass_3(3, 1)
-        pass_2(2, 1)
         pass_0(3, 1)
         after_pass_0(3, 1)
+        store(1)
+        pass_2(2, 1)
+        empty(2)
         pass_3(3, 0)
         pass_3(3, 1)
+        store(2)
         pass_1(3, 0)
         pass_1(3, 1)
         pass_2(3, 0)

@@ -43,7 +43,7 @@ def tile_fast2order_de_conv_kernel(tc, x, W_words, W_scales, out):
         pair_pool = ctx.enter_context(tc.tile_pool(name="pairs", bufs=1))
         below_pool = ctx.enter_context(tc.tile_pool(name="below", bufs=4))
         above_pool = ctx.enter_context(tc.tile_pool(name="above", bufs=4))
-        code_pool = ctx.enter_context(tc.tile_pool(name="code", bufs=4))
+        code_pool = ctx.enter_context(tc.tile_pool(name="code", bufs=8))
         stage_pool = ctx.enter_context(tc.tile_pool(name="stage", bufs=4))
         psum = ctx.enter_context(tc.psum_pool(name="acc", bufs=2))
 
@@ -59,20 +59,26 @@ def tile_fast2order_de_conv_kernel(tc, x, W_words, W_scales, out):
                 x_above.append(keep.tile([P, ABOVE_ROWS, SIDE], BF16, name="x_above%d" % b))
         x_left_above0 = keep.tile([P, PIXELS], BF16, name="x_left_above0")
 
-        nc.vector.memset(w_scales[:].rearrange("p a n -> p (a n)").bitcast(I32), 0)
-        for b in range(IMAGES):
-            nc.gpsimd.memset(x_below[b][:, SIDE - WINDOW + 1 : SIDE, :], 0)
-            if b < LAST:
-                nc.gpsimd.memset(x_above[b][:, 0 : WINDOW - 1, :], 0)
-
         pixels = x.rearrange("b c h w -> b c (h w)")
 
-        def load_left_lane(tile, source, s):
+        def load_left_lane(tile, source, s, queue=nc.sync):
             for icl in range(2):
-                nc.sync.dma_start(
+                queue.dma_start(
                     out=tile[4 * icl + s : P : 8, 0 : PIXELS - 1],
                     in_=pixels[source, :, icl : icl + PIXELS - 1],
                 )
+
+        def load_left(b, queue=nc.sync):
+            for s in range(WINDOW):
+                load_left_lane(x_left[b], b, s, queue)
+
+        load_left(LAST, nc.gpsimd)
+
+        nc.vector.memset(w_scales[:].rearrange("p a n -> p (a n)").bitcast(I32), 0)
+        for b in range(IMAGES):
+            nc.vector.memset(x_below[b][:, SIDE - WINDOW + 1 : SIDE, :], 0)
+            if b < LAST:
+                nc.vector.memset(x_above[b][:, 0 : WINDOW - 1, :], 0)
 
         def load_rows(tile, source, s, image_row, tile_row, count):
             nc.sync.dma_start(
@@ -81,10 +87,6 @@ def tile_fast2order_de_conv_kernel(tc, x, W_words, W_scales, out):
                 .unsqueeze(1)
                 .to_broadcast([CHANNELS, 2, count * SIDE]),
             )
-
-        def load_left(b):
-            for s in range(WINDOW):
-                load_left_lane(x_left[b], b, s)
 
         def load_below(b):
             for s in range(WINDOW):
@@ -174,7 +176,7 @@ def tile_fast2order_de_conv_kernel(tc, x, W_words, W_scales, out):
                         op=mybir.AluOpType.mult,
                     )
 
-        def join(products, pairs, ich, first_row):
+        def join(copy, products, pairs, ich, first_row):
             slot, distance = JOIN_SLOTS[ich]
             halves = (
                 pairs[:, first_row:SIDE, :, slot : slot + 2 * distance, :]
@@ -182,7 +184,7 @@ def tile_fast2order_de_conv_kernel(tc, x, W_words, W_scales, out):
                 .bitcast(F32)
                 .rearrange("p a (f s) -> p a s f", f=2)
             )
-            nc.scalar.copy(
+            copy(
                 out=products[:, first_row:SIDE]
                 .rearrange("p u h k -> p (u h k)")
                 .bitcast(F32)
@@ -202,21 +204,23 @@ def tile_fast2order_de_conv_kernel(tc, x, W_words, W_scales, out):
                 pairs_below[b] = pair_pool.tile([P, SIDE, 2, SLOTS, 2], BF16, name="pairs_below", align_bytes=64)
             multiply(pairs_below[b], doubled_below[b], x_below[b], 0, runs)
 
-        def multiply_above(b):
+        def multiply_above(b, runs=PAIR_RUNS):
             pairs_above[b] = pairs_shared
-            multiply(pairs_above[b], doubled_above[b], x_above[b], 1)
+            multiply(pairs_above[b], doubled_above[b], x_above[b], 1, runs)
+
+        def park(b):
             move_lane(pairs_last, b + 1, pairs_shared, 0, 1, SIDE - 1)
             if b + 1 == LAST:
                 move_lane(pairs_last, 0, pairs_shared, 0, 1, SIDE - 1)
                 pairs_above[LAST] = pairs_last
 
-        def join_below(b, ich):
+        def join_below(b, ich, copy=nc.scalar.copy):
             below[(b, ich)] = below_pool.tile([P, SIDE, 2, 2 * GRID], BF16, name="below", align_bytes=64)
-            join(below[(b, ich)], pairs_below[b], ich, 0)
+            join(copy, below[(b, ich)], pairs_below[b], ich, 0)
 
-        def join_above(b, ich):
+        def join_above(b, ich, copy=nc.scalar.copy):
             above[(b, ich)] = above_pool.tile([P, SIDE, 2, 2 * GRID], BF16, name="above", align_bytes=64)
-            join(above[(b, ich)], pairs_above[b], ich, 1)
+            join(copy, above[(b, ich)], pairs_above[b], ich, 1)
 
         def contract(b, ich, ir, products):
             codes = code_pool.tile([P, POSITIONS], U32, name="codes", align_bytes=64)
@@ -319,11 +323,13 @@ def tile_fast2order_de_conv_kernel(tc, x, W_words, W_scales, out):
         load_x(1)
         load_weights(0, 1)
         load_weights(0, 3)
+        first, second, third = PAIR_RUNS[:1], PAIR_RUNS[1:2], PAIR_RUNS[2:]
         multiply_below(0)
         join_below(0, 0)
         join_below(0, 1)
         double_above(nc.vector.tensor_copy, 0, x_left_above0)
         multiply_above(0)
+        park(0)
         double_below(nc.scalar.copy, 1)
         prepare_above(1)
         pass_0(0, 0)
@@ -334,82 +340,90 @@ def tile_fast2order_de_conv_kernel(tc, x, W_words, W_scales, out):
         join_above(0, 1)
         after_pass_0(0, 1)
         before_pass_3(0, 1)
+        load_left(2)
         load_weights(1, 1)
         load_weights(1, 3)
-        load_x(2)
+        load_below(2)
 
         multiply_below(1)
         join_below(1, 0)
         join_below(1, 1)
         double_above(nc.vector.tensor_copy, 1, x_left[1])
         pass_1(0, 0)
-        pass_3(0, 0)
+        multiply_above(1, first)
         load_weights(0, 2)
-        load_left(3)
-        multiply_above(1)
-        join_above(1, 0)
-        before_pass_3(1, 0)
+        pass_3(0, 0)
+        double_below(nc.scalar.copy, 2)
+        multiply_above(1, second)
         pass_1(0, 1)
+        multiply_above(1, third)
+        park(1)
+        join_above(1, 0)
         pass_3(0, 1)
-        join_above(1, 1)
+        before_pass_3(1, 0)
         load_weights(1, 2)
+        join_above(1, 1)
         pass_0(1, 0)
         after_pass_0(1, 0)
-        double_below(nc.scalar.copy, 2)
-        pass_0(1, 1)
         before_pass_3(1, 1)
+        pass_2(0, 0)
+        pass_0(1, 1)
         after_pass_0(1, 1)
         load_x_above(2)
-        pass_2(0, 0)
         double_below(nc.scalar.copy, 3)
         pass_2(0, 1)
         empty(0)
 
-        multiply_below(2)
+        multiply_below(2, first)
+        multiply_below(2, second)
+        pass_1(1, 0)
+        multiply_below(2, third)
         turn_above(2)
-        load_below(3)
         join_below(2, 0)
         join_below(2, 1)
-        pass_1(1, 0)
         pass_3(1, 0)
-        pass_1(1, 1)
         store(0)
-        multiply_above(2)
+        pass_1(1, 1)
+        pass_3(1, 1)
+        load_below(3)
+        multiply_above(2, first)
+        pass_0(2, 0)
+        multiply_above(2, second)
+        pass_2(1, 0)
+        multiply_above(2, third)
+        park(2)
         join_above(2, 0)
         before_pass_3(2, 0)
-        pass_3(1, 1)
-        join_above(2, 1)
-        pass_0(2, 0)
         after_pass_0(2, 0)
+        join_above(2, 1)
         before_pass_3(2, 1)
+        pass_2(1, 1)
         pass_0(2, 1)
         after_pass_0(2, 1)
-        pass_2(1, 0)
-        pass_2(1, 1)
+        empty(1)
 
         multiply_below(3)
-        join_above(3, 0)
         join_below(3, 0)
-        join_above(3, 1)
-        before_pass_3(3, 0)
+        join_above(3, 0)
         join_below(3, 1)
-        empty(1)
         pass_1(2, 0)
         pass_3(2, 0)
-        before_pass_3(3, 1)
         pass_1(2, 1)
         pass_3(2, 1)
+        join_above(3, 1, nc.vector.tensor_copy)
+        store(1)
+        before_pass_3(3, 0)
+        before_pass_3(3, 1)
         pass_0(3, 0)
         after_pass_0(3, 0)
         pass_2(2, 0)
-        pass_0(3, 1)
-        after_pass_0(3, 1)
-        store(1)
         pass_2(2, 1)
         empty(2)
+        pass_0(3, 1)
+        after_pass_0(3, 1)
         pass_3(3, 0)
-        pass_3(3, 1)
         store(2)
+        pass_3(3, 1)
         pass_1(3, 0)
         pass_1(3, 1)
         pass_2(3, 0)

@@ -222,16 +222,11 @@ def tile_fast2order_de_conv_kernel(tc, x, W_words, W_scales, out):
             above[(b, ich)] = above_pool.tile([P, SIDE, 2, 2 * GRID], BF16, name="above", align_bytes=64)
             join(copy, above[(b, ich)], pairs_above[b], ich, 1)
 
-        def contract(b, ich, ir, products):
+        def contract(b, ich, ir, products, part=(0, 1)):
+            rows = GRID // HALVES
+            last = ich == 1 and ir == 2
             codes = code_pool.tile([P, POSITIONS], U32, name="codes", align_bytes=64)
             scales = code_pool.tile([P, POSITIONS], U8, name="scales", align_bytes=64)
-            last = ich == 1 and ir == 2
-            parts = [[0], [1]] if last and b == LAST else [[0, 1]]
-            for part in parts:
-                contract_halves(b, ich, ir, products, codes, scales, part, last)
-
-        def contract_halves(b, ich, ir, products, codes, scales, part, last):
-            rows = GRID // HALVES
             columns = slice(N_TILE * part[0], N_TILE * (part[-1] + 1))
             nc.vector.quantize_mx(
                 out=codes[:, columns].bitcast(FP8X4),
@@ -302,8 +297,8 @@ def tile_fast2order_de_conv_kernel(tc, x, W_words, W_scales, out):
             contract(b, ich, 3, above[(b, ich)])
             move_lane(above[(b, ich)], 1, below[(b, ich)], 1, 2, GRID + 1)
 
-        def pass_2(b, ich):
-            contract(b, ich, 2, above[(b, ich)])
+        def pass_2(b, ich, part=(0, 1)):
+            contract(b, ich, 2, above[(b, ich)], part)
 
         load_x(0)
         doubled_below[0] = new_doubled("doubled_below")
@@ -324,16 +319,16 @@ def tile_fast2order_de_conv_kernel(tc, x, W_words, W_scales, out):
         load_weights(0, 1)
         load_weights(0, 3)
         first, second, third = PAIR_RUNS[:1], PAIR_RUNS[1:2], PAIR_RUNS[2:]
+        double_above(nc.scalar.copy, 0, x_left_above0)
         multiply_below(0)
         join_below(0, 0)
         join_below(0, 1)
-        double_above(nc.vector.tensor_copy, 0, x_left_above0)
         multiply_above(0)
         park(0)
         double_below(nc.scalar.copy, 1)
         prepare_above(1)
         pass_0(0, 0)
-        join_above(0, 0)
+        join_above(0, 0, nc.vector.tensor_copy)
         after_pass_0(0, 0)
         before_pass_3(0, 0)
         pass_0(0, 1)
@@ -346,18 +341,18 @@ def tile_fast2order_de_conv_kernel(tc, x, W_words, W_scales, out):
         load_below(2)
 
         multiply_below(1)
+        double_above(nc.scalar.copy, 1, x_left[1])
         join_below(1, 0)
         join_below(1, 1)
-        double_above(nc.vector.tensor_copy, 1, x_left[1])
         pass_1(0, 0)
-        multiply_above(1, first)
-        load_weights(0, 2)
         pass_3(0, 0)
-        double_below(nc.scalar.copy, 2)
+        load_weights(0, 2)
+        multiply_above(1, first)
         multiply_above(1, second)
         pass_1(0, 1)
         multiply_above(1, third)
         park(1)
+        double_below(nc.scalar.copy, 2)
         join_above(1, 0)
         pass_3(0, 1)
         before_pass_3(1, 0)
@@ -371,10 +366,10 @@ def tile_fast2order_de_conv_kernel(tc, x, W_words, W_scales, out):
         after_pass_0(1, 1)
         load_x_above(2)
         double_below(nc.scalar.copy, 3)
-        pass_2(0, 1)
-        empty(0)
 
         multiply_below(2, first)
+        pass_2(0, 1)
+        empty(0)
         multiply_below(2, second)
         pass_1(1, 0)
         multiply_below(2, third)
@@ -426,5 +421,6 @@ def tile_fast2order_de_conv_kernel(tc, x, W_words, W_scales, out):
         pass_3(3, 1)
         pass_1(3, 0)
         pass_1(3, 1)
-        pass_2(3, 0)
-        pass_2(3, 1)
+        for h in range(HALVES):
+            pass_2(3, 0, (h,))
+            pass_2(3, 1, (h,))

@@ -20,9 +20,12 @@ PIXELS = SIDE * SIDE
 GRID = 32
 WINDOW = 4
 LEFT_PAIRS = 17
-PAIR_RUNS = ((0, 16, 0, 17), (-1, 36, 1, 16), (1, 0, 0, 16))
-SLOTS = 56
-GAPS = ((33, 3), (52, 4))
+ROW_PAIRS = 2 * LEFT_PAIRS
+HEAD = 16
+TAIL = 48
+FILLED_TAIL = 12
+RUN = SIDE * LEFT_PAIRS * 2
+RUNS = 6
 SPLIT_ROW = 20
 JOIN_SLOTS = ((16, 20), (0, 17))
 OUT_CH = 256
@@ -39,8 +42,6 @@ def tile_fast2order_de_conv_kernel(tc, x, W_words, W_scales, out):
     with ExitStack() as ctx:
         ctx.enter_context(tc.manual_schedule())
         keep = ctx.enter_context(tc.tile_pool(name="keep", bufs=1))
-        doubled_pool = ctx.enter_context(tc.tile_pool(name="doubled", bufs=2))
-        pair_pool = ctx.enter_context(tc.tile_pool(name="pairs", bufs=1))
         below_pool = ctx.enter_context(tc.tile_pool(name="below", bufs=4))
         above_pool = ctx.enter_context(tc.tile_pool(name="above", bufs=4))
         code_pool = ctx.enter_context(tc.tile_pool(name="code", bufs=8))
@@ -132,91 +133,108 @@ def tile_fast2order_de_conv_kernel(tc, x, W_words, W_scales, out):
                 out=lane(target, to, first_row, last_row), in_=lane(source, s, first_row, last_row)
             )
 
+        doubled_tiles = []
+        for n in range(4):
+            doubled = keep.tile([P, HEAD + SIDE * 2 * ROW_PAIRS + TAIL], BF16, name="doubled%d" % n)
+            nc.vector.memset(doubled[:, 0:HEAD], 0)
+            nc.vector.memset(doubled[:, HEAD + SIDE * 2 * ROW_PAIRS :][:, 0:FILLED_TAIL], 0)
+            doubled_tiles.append(doubled)
         doubled_below = {}
         doubled_above = {}
 
-        def new_doubled(name):
-            return doubled_pool.tile([P, SIDE, 2, LEFT_PAIRS, 2], BF16, name=name)
-
-        def double_left(copy, tile, source, first_row, last_row):
+        def double_left(copy, doubled, source, first_row, last_row):
             rows = source[:].rearrange("p (u w) -> p u w", w=SIDE)[:, first_row : last_row + 1, 0 : 2 * LEFT_PAIRS]
+            width = 2 * ROW_PAIRS
             copy(
-                out=tile[:, first_row : last_row + 1],
+                out=doubled[:, HEAD + width * first_row : HEAD + width * (last_row + 1)].rearrange(
+                    "p (u h q e) -> p u h q e", h=2, q=LEFT_PAIRS, e=2
+                ),
                 in_=rows.rearrange("p u (q h) -> p u h q", h=2)
                 .unsqueeze(4)
                 .to_broadcast([P, last_row + 1 - first_row, 2, LEFT_PAIRS, 2]),
             )
 
         def double_below(copy, b):
-            doubled_below[b] = new_doubled("doubled_below")
+            doubled_below[b] = doubled_tiles[b % 2]
             double_left(copy, doubled_below[b], x_left[b], 0, SIDE - 1)
 
+        def double_above(copy, b, source):
+            doubled_above[b] = doubled_tiles[2 + b]
+            double_left(copy, doubled_above[b], source, 0, SIDE - 1)
+
         def turn_above(b):
-            move_lane(doubled_below[b], 0, doubled_below[LAST], 0, 1, SIDE - 1)
+            first, last = HEAD + 2 * ROW_PAIRS, HEAD + SIDE * 2 * ROW_PAIRS + FILLED_TAIL
+            nc.sync.dma_start(
+                out=doubled_below[b][0:P:WINDOW, first:last], in_=doubled_below[LAST][0:P:WINDOW, first:last]
+            )
             doubled_above[b] = doubled_below[b]
 
-        def double_above(copy, b, source):
-            doubled_above[b] = new_doubled("doubled_above")
-            double_left(copy, doubled_above[b], source, 1, SIDE - 1)
+        def multiply(pairs, doubled, right, first_row, js):
+            for j in js:
+                for h in range(2):
+                    start = RUN * (2 * (1 - j) + h)
+                    left = HEAD + 2 * (LEFT_PAIRS * h + j)
+                    nc.vector.tensor_tensor(
+                        out=pairs[:, start : start + RUN].rearrange("p (u k) -> p u k", k=2 * LEFT_PAIRS)[
+                            :, first_row:SIDE
+                        ],
+                        in0=doubled[:, left : left + SIDE * 2 * ROW_PAIRS].rearrange(
+                            "p (u k) -> p u k", k=2 * ROW_PAIRS
+                        )[:, first_row:SIDE, 0 : 2 * LEFT_PAIRS],
+                        in1=right[:, first_row:SIDE, h : h + 2 * LEFT_PAIRS],
+                        op=mybir.AluOpType.mult,
+                    )
+
+        def join(copy, products, pairs, ich, first_row):
+            apart = 2 * RUN + 2
+            start = 2 * RUN * (1 - ich)
+            halves = (
+                pairs[:, start : start + 2 * apart]
+                .bitcast(F32)
+                .rearrange("p (f a) -> p f a", f=2)[:, :, 0:RUN]
+                .rearrange("p f (h u q) -> p u h q f", h=2, q=LEFT_PAIRS)
+            )
+            copy(
+                out=products[:, first_row:SIDE]
+                .rearrange("p u h k -> p (u h k)")
+                .bitcast(F32)
+                .rearrange("p (u h q f) -> p u h q f", h=2, q=GRID // 2, f=2),
+                in_=halves[:, first_row:SIDE, :, 0 : GRID // 2, :],
+            )
+
+        def new_pairs(name):
+            return keep.tile([P, RUNS * RUN + 4], BF16, name=name, align_bytes=64)
+
+        pairs_of_below = new_pairs("pairs_of_below")
+        pairs_of_above = new_pairs("pairs_of_above")
+        pairs_last = new_pairs("pairs_last")
+        for pairs in (pairs_of_below, pairs_of_above, pairs_last):
+            nc.vector.memset(pairs[:, RUNS * RUN :], 0)
+        pairs_above = {LAST: pairs_last}
 
         below = {}
         above = {}
         acc = {}
         opened = set()
 
-        def multiply(pairs, doubled, right, first_row, runs=PAIR_RUNS):
-            for j, slot, first_q, count in runs:
-                for h in range(2):
-                    nc.vector.tensor_tensor(
-                        out=pairs[:, first_row:SIDE, h, slot : slot + count, :].rearrange("p u q e -> p u (q e)"),
-                        in0=doubled[:, first_row:SIDE, h, first_q + j : first_q + j + count, :].rearrange(
-                            "p u q e -> p u (q e)"
-                        ),
-                        in1=right[:, first_row:SIDE, h + 2 * first_q : h + 2 * (first_q + count)],
-                        op=mybir.AluOpType.mult,
-                    )
+        def multiply_below(b, js=(0, -1, 1)):
+            multiply(pairs_of_below, doubled_below[b], x_below[b], 0, js)
 
-        def join(copy, products, pairs, ich, first_row):
-            slot, distance = JOIN_SLOTS[ich]
-            halves = (
-                pairs[:, first_row:SIDE, :, slot : slot + 2 * distance, :]
-                .rearrange("p u h s e -> p (u h) (s e)")
-                .bitcast(F32)
-                .rearrange("p a (f s) -> p a s f", f=2)
-            )
-            copy(
-                out=products[:, first_row:SIDE]
-                .rearrange("p u h k -> p (u h k)")
-                .bitcast(F32)
-                .rearrange("p (a q f) -> p a q f", q=GRID // 2, f=2),
-                in_=halves[:, :, 0 : GRID // 2, :],
-            )
-
-        pairs_below = {}
-        pairs_above = {}
-        pairs_shared = keep.tile([P, SIDE, 2, SLOTS, 2], BF16, name="pairs_shared", align_bytes=64)
-        pairs_last = keep.tile([P, SIDE, 2, SLOTS, 2], BF16, name="pairs_last", align_bytes=64)
-        for slot, count in GAPS:
-            nc.vector.memset(pairs_shared[:, :, :, slot : slot + count, :], 0)
-
-        def multiply_below(b, runs=PAIR_RUNS):
-            if b not in pairs_below:
-                pairs_below[b] = pair_pool.tile([P, SIDE, 2, SLOTS, 2], BF16, name="pairs_below", align_bytes=64)
-            multiply(pairs_below[b], doubled_below[b], x_below[b], 0, runs)
-
-        def multiply_above(b, runs=PAIR_RUNS):
-            pairs_above[b] = pairs_shared
-            multiply(pairs_above[b], doubled_above[b], x_above[b], 1, runs)
+        def multiply_above(b, js=(0, -1, 1)):
+            pairs_above[b] = pairs_of_above
+            multiply(pairs_of_above, doubled_above[b], x_above[b], 1, js)
 
         def park(b):
-            move_lane(pairs_last, b + 1, pairs_shared, 0, 1, SIDE - 1)
-            if b + 1 == LAST:
-                move_lane(pairs_last, 0, pairs_shared, 0, 1, SIDE - 1)
-                pairs_above[LAST] = pairs_last
+            for to in (b + 1, 0) if b + 1 == LAST else (b + 1,):
+                target, source = [
+                    tile[s:P:WINDOW, 0 : RUNS * RUN].rearrange("p (r k) -> p r k", r=RUNS)[:, :, 2 * LEFT_PAIRS :]
+                    for tile, s in ((pairs_last, to), (pairs_of_above, 0))
+                ]
+                nc.sync.dma_start(out=target, in_=source)
 
         def join_below(b, ich, copy=nc.scalar.copy):
             below[(b, ich)] = below_pool.tile([P, SIDE, 2, 2 * GRID], BF16, name="below", align_bytes=64)
-            join(copy, below[(b, ich)], pairs_below[b], ich, 0)
+            join(copy, below[(b, ich)], pairs_of_below, ich, 0)
 
         def join_above(b, ich, copy=nc.scalar.copy):
             above[(b, ich)] = above_pool.tile([P, SIDE, 2, 2 * GRID], BF16, name="above", align_bytes=64)
@@ -301,7 +319,7 @@ def tile_fast2order_de_conv_kernel(tc, x, W_words, W_scales, out):
             contract(b, ich, 2, above[(b, ich)], part)
 
         load_x(0)
-        doubled_below[0] = new_doubled("doubled_below")
+        doubled_below[0] = doubled_tiles[0]
         double_left(nc.vector.tensor_copy, doubled_below[0], x_left[0], 0, SPLIT_ROW - 1)
         double_left(nc.scalar.copy, doubled_below[0], x_left[0], SPLIT_ROW, SIDE - 1)
         for s in range(WINDOW):
@@ -318,7 +336,7 @@ def tile_fast2order_de_conv_kernel(tc, x, W_words, W_scales, out):
         load_x(1)
         load_weights(0, 1)
         load_weights(0, 3)
-        first, second, third = PAIR_RUNS[:1], PAIR_RUNS[1:2], PAIR_RUNS[2:]
+        first, second, third = (0,), (-1,), (1,)
         double_above(nc.scalar.copy, 0, x_left_above0)
         multiply_below(0)
         join_below(0, 0)
@@ -381,18 +399,16 @@ def tile_fast2order_de_conv_kernel(tc, x, W_words, W_scales, out):
         pass_1(1, 1)
         pass_3(1, 1)
         load_below(3)
-        multiply_above(2, first)
-        pass_0(2, 0)
-        multiply_above(2, second)
-        pass_2(1, 0)
-        multiply_above(2, third)
+        multiply_above(2)
         park(2)
         join_above(2, 0)
+        pass_0(2, 0)
+        pass_2(1, 0)
         before_pass_3(2, 0)
         after_pass_0(2, 0)
         join_above(2, 1)
-        before_pass_3(2, 1)
         pass_2(1, 1)
+        before_pass_3(2, 1)
         pass_0(2, 1)
         after_pass_0(2, 1)
         empty(1)
@@ -405,7 +421,7 @@ def tile_fast2order_de_conv_kernel(tc, x, W_words, W_scales, out):
         pass_3(2, 0)
         pass_1(2, 1)
         pass_3(2, 1)
-        join_above(3, 1, nc.vector.tensor_copy)
+        join_above(3, 1)
         store(1)
         before_pass_3(3, 0)
         before_pass_3(3, 1)

from contextlib import ExitStack

import concourse.mybir as mybir

FLOPS = 2 * 4096 * 4096 * 256

BF16 = mybir.dt.bfloat16
F32 = mybir.dt.float32
I32 = mybir.dt.int32
U8 = mybir.dt.uint8
U32 = mybir.dt.uint32
FP8X4 = mybir.dt.float8_e4m3fn_x4

P = 128
IMAGES = 4
LAST = IMAGES - 1
CHANNELS = 16
SIDE = 35
PIXELS = SIDE * SIDE
GRID = 32
WINDOW = 4
LEFT_PAIRS = 17
ROW_PAIRS = 2 * LEFT_PAIRS
HEAD = 16
TAIL = 48
FILLED_TAIL = 12
RUN = SIDE * LEFT_PAIRS * 2
RUNS = 6
SPLIT_ROW = 20
JOIN_SLOTS = ((16, 20), (0, 17))
OUT_CH = 256
M_TILE = 128
N_TILE = 512
POSITIONS = GRID * GRID
HALVES = POSITIONS // N_TILE
ABOVE_ROWS = SIDE + WINDOW - 1
PASSES = 8


def tile_fast2order_de_conv_kernel(tc, x, W_words, W_scales, out):
    nc = tc.nc
    with ExitStack() as ctx:
        ctx.enter_context(tc.manual_schedule())
        keep = ctx.enter_context(tc.tile_pool(name="keep", bufs=1))
        below_pool = ctx.enter_context(tc.tile_pool(name="below", bufs=4))
        above_pool = ctx.enter_context(tc.tile_pool(name="above", bufs=4))
        code_pool = ctx.enter_context(tc.tile_pool(name="code", bufs=8))
        stage_pool = ctx.enter_context(tc.tile_pool(name="stage", bufs=4))
        psum = ctx.enter_context(tc.psum_pool(name="acc", bufs=2))

        w_words = keep.tile([P, PASSES, OUT_CH * WINDOW], U8, name="w_words", align_bytes=64)
        w_scales = keep.tile([P, PASSES, OUT_CH], U8, name="w_scales", align_bytes=64)
        x_left = []
        x_below = []
        x_above = []
        for b in range(IMAGES):
            x_left.append(keep.tile([P, PIXELS], BF16, name="x_left%d" % b))
            x_below.append(keep.tile([P, SIDE, SIDE], BF16, name="x_below%d" % b))
            if b < LAST:
                x_above.append(keep.tile([P, ABOVE_ROWS, SIDE], BF16, name="x_above%d" % b))
        x_left_above0 = keep.tile([P, PIXELS], BF16, name="x_left_above0")

        pixels = x.rearrange("b c h w -> b c (h w)")

        def load_left_lane(tile, source, s, queue=nc.sync):
            for icl in range(2):
                queue.dma_start(
                    out=tile[4 * icl + s : P : 8, 0 : PIXELS - 1],
                    in_=pixels[source, :, icl : icl + PIXELS - 1],
                )

        def load_left(b, queue=nc.sync):
            for s in range(WINDOW):
                load_left_lane(x_left[b], b, s, queue)

        load_left(LAST, nc.gpsimd)

        nc.vector.memset(w_scales[:].rearrange("p a n -> p (a n)").bitcast(I32), 0)
        for b in range(IMAGES):
            nc.vector.memset(x_below[b][:, SIDE - WINDOW + 1 : SIDE, :], 0)
            if b < LAST:
                nc.vector.memset(x_above[b][:, 0 : WINDOW - 1, :], 0)

        def load_rows(tile, source, s, image_row, tile_row, count):
            nc.sync.dma_start(
                out=tile[s:P:WINDOW, tile_row : tile_row + count, :].rearrange("p h w -> p (h w)"),
                in_=pixels[source, :, image_row * SIDE : (image_row + count) * SIDE]
                .unsqueeze(1)
                .to_broadcast([CHANNELS, 2, count * SIDE]),
            )

        def load_below(b):
            for s in range(WINDOW):
                load_rows(x_below[b], b, s, s, 0, SIDE - s)

        def load_x(b):
            load_left(b)
            load_below(b)

        def load_x_above(b):
            for s in range(WINDOW):
                drop = WINDOW - s if s > 0 else LAST - b
                load_rows(x_above[b], b if s > 0 else LAST, s, 0, drop, SIDE)

        def prepare_above(b):
            load_left_lane(x_left[b], LAST, 0)
            load_x_above(b)

        word_rows = (
            W_words.rearrange("g p n t -> (g p) (n t)")
            .bitcast(I32)
            .rearrange("(c a l j) w -> a j c l w", a=PASSES, l=2, j=WINDOW)
        )
        word_rows_in_order = (
            W_words.rearrange("g p n t -> (g p) (n t)").bitcast(I32).rearrange("(c a q) w -> a c q w", a=PASSES, q=8)
        )

        def load_weights(ich, ir):
            a = 2 * ir + ich
            if ir == 0:
                nc.sync.dma_start(out=w_words[:, a, :].bitcast(I32), in_=word_rows_in_order[a])
            else:
                for s in range(WINDOW):
                    nc.sync.dma_start(
                        out=w_words[s:P:WINDOW, a, :].bitcast(I32), in_=word_rows[a, (s + ir) % WINDOW]
                    )

        def lane(tile, s, first_row, last_row):
            return tile[s:P:WINDOW, first_row : last_row + 1]

        def move_lane(target, to, source, s, first_row, last_row):
            nc.sync.dma_start(
                out=lane(target, to, first_row, last_row), in_=lane(source, s, first_row, last_row)
            )

        doubled_tiles = []
        for n in range(4):
            doubled = keep.tile([P, HEAD + SIDE * 2 * ROW_PAIRS + TAIL], BF16, name="doubled%d" % n)
            nc.vector.memset(doubled[:, 0:HEAD], 0)
            nc.vector.memset(doubled[:, HEAD + SIDE * 2 * ROW_PAIRS :][:, 0:FILLED_TAIL], 0)
            doubled_tiles.append(doubled)
        doubled_below = {}
        doubled_above = {}

        def double_left(copy, doubled, source, first_row, last_row):
            rows = source[:].rearrange("p (u w) -> p u w", w=SIDE)[:, first_row : last_row + 1, 0 : 2 * LEFT_PAIRS]
            width = 2 * ROW_PAIRS
            copy(
                out=doubled[:, HEAD + width * first_row : HEAD + width * (last_row + 1)].rearrange(
                    "p (u h q e) -> p u h q e", h=2, q=LEFT_PAIRS, e=2
                ),
                in_=rows.rearrange("p u (q h) -> p u h q", h=2)
                .unsqueeze(4)
                .to_broadcast([P, last_row + 1 - first_row, 2, LEFT_PAIRS, 2]),
            )

        def double_below(copy, b):
            doubled_below[b] = doubled_tiles[b % 2]
            double_left(copy, doubled_below[b], x_left[b], 0, SIDE - 1)

        def double_above(copy, b, source):
            doubled_above[b] = doubled_tiles[2 + b]
            double_left(copy, doubled_above[b], source, 0, SIDE - 1)

        def turn_above(b):
            first, last = HEAD + 2 * ROW_PAIRS, HEAD + SIDE * 2 * ROW_PAIRS + FILLED_TAIL
            nc.sync.dma_start(
                out=doubled_below[b][0:P:WINDOW, first:last], in_=doubled_below[LAST][0:P:WINDOW, first:last]
            )
            doubled_above[b] = doubled_below[b]

        def multiply(pairs, doubled, right, first_row, js):
            for j in js:
                for h in range(2):
                    start = RUN * (2 * (1 - j) + h)
                    left = HEAD + 2 * (LEFT_PAIRS * h + j)
                    nc.vector.tensor_tensor(
                        out=pairs[:, start : start + RUN].rearrange("p (u k) -> p u k", k=2 * LEFT_PAIRS)[
                            :, first_row:SIDE
                        ],
                        in0=doubled[:, left : left + SIDE * 2 * ROW_PAIRS].rearrange(
                            "p (u k) -> p u k", k=2 * ROW_PAIRS
                        )[:, first_row:SIDE, 0 : 2 * LEFT_PAIRS],
                        in1=right[:, first_row:SIDE, h : h + 2 * LEFT_PAIRS],
                        op=mybir.AluOpType.mult,
                    )

        def join(copy, products, pairs, ich, first_row):
            apart = 2 * RUN + 2
            start = 2 * RUN * (1 - ich)
            halves = (
                pairs[:, start : start + 2 * apart]
                .bitcast(F32)
                .rearrange("p (f a) -> p f a", f=2)[:, :, 0:RUN]
                .rearrange("p f (h u q) -> p u h q f", h=2, q=LEFT_PAIRS)
            )
            copy(
                out=products[:, first_row:SIDE]
                .rearrange("p u h k -> p (u h k)")
                .bitcast(F32)
                .rearrange("p (u h q f) -> p u h q f", h=2, q=GRID // 2, f=2),
                in_=halves[:, first_row:SIDE, :, 0 : GRID // 2, :],
            )

        def new_pairs(name):
            return keep.tile([P, RUNS * RUN + 4], BF16, name=name, align_bytes=64)

        pairs_of_below = new_pairs("pairs_of_below")
        pairs_of_above = new_pairs("pairs_of_above")
        pairs_last = new_pairs("pairs_last")
        for pairs in (pairs_of_below, pairs_of_above, pairs_last):
            nc.vector.memset(pairs[:, RUNS * RUN :], 0)
        pairs_above = {LAST: pairs_last}

        below = {}
        above = {}
        acc = {}
        opened = set()

        def multiply_below(b, js=(0, -1, 1)):
            multiply(pairs_of_below, doubled_below[b], x_below[b], 0, js)

        def multiply_above(b, js=(0, -1, 1)):
            pairs_above[b] = pairs_of_above
            multiply(pairs_of_above, doubled_above[b], x_above[b], 1, js)

        def park(b):
            for to in (b + 1, 0) if b + 1 == LAST else (b + 1,):
                target, source = [
                    tile[s:P:WINDOW, 0 : RUNS * RUN].rearrange("p (r k) -> p r k", r=RUNS)[:, :, 2 * LEFT_PAIRS :]
                    for tile, s in ((pairs_last, to), (pairs_of_above, 0))
                ]
                nc.sync.dma_start(out=target, in_=source)

        def join_below(b, ich, copy=nc.scalar.copy):
            below[(b, ich)] = below_pool.tile([P, SIDE, 2, 2 * GRID], BF16, name="below", align_bytes=64)
            join(copy, below[(b, ich)], pairs_of_below, ich, 0)

        def join_above(b, ich, copy=nc.scalar.copy):
            above[(b, ich)] = above_pool.tile([P, SIDE, 2, 2 * GRID], BF16, name="above", align_bytes=64)
            join(copy, above[(b, ich)], pairs_above[b], ich, 1)

        def contract(b, ich, ir, products, part=(0, 1)):
            rows = GRID // HALVES
            last = ich == 1 and ir == 2
            codes = code_pool.tile([P, POSITIONS], U32, name="codes", align_bytes=64)
            scales = code_pool.tile([P, POSITIONS], U8, name="scales", align_bytes=64)
            columns = slice(N_TILE * part[0], N_TILE * (part[-1] + 1))
            nc.vector.quantize_mx(
                out=codes[:, columns].bitcast(FP8X4),
                scales=scales[:, columns],
                in_=products[:, ir + rows * part[0] : ir + rows * (part[-1] + 1)].rearrange("p u h k -> p (u h k)"),
            )
            first = b not in opened
            opened.add(b)
            a = 2 * ir + ich
            for oh in range(OUT_CH // M_TILE):
                for h in part:
                    if first:
                        acc[(b, oh, h)] = psum.tile([M_TILE, N_TILE], F32, name="acc%d%d" % (oh, h))
                    nc.tensor.matmul_mx(
                        out=acc[(b, oh, h)][:],
                        lhsT=w_words[:, a, 4 * M_TILE * oh : 4 * M_TILE * (oh + 1)].bitcast(FP8X4),
                        lhsT_scale=w_scales[:, a, M_TILE * oh : M_TILE * (oh + 1)],
                        rhs=codes[:, N_TILE * h : N_TILE * (h + 1)].bitcast(FP8X4),
                        rhs_scale=scales[:, N_TILE * h : N_TILE * (h + 1)],
                        start=first,
                        stop=last,
                    )
            if last and b == LAST:
                for oh in range(OUT_CH // M_TILE):
                    for h in part:
                        empty_bank(nc.vector.tensor_copy if oh == 0 and h == 1 else nc.scalar.copy, b, oh, h)
                        store_bank(b, oh, h)

        staged = {}

        def empty_bank(copy, b, oh, h):
            stage = stage_pool.tile([M_TILE, GRID // HALVES, GRID // 2, 2], F32, name="stage")
            copy(out=stage[:], in_=acc[(b, oh, h)][:].rearrange("p (y h q) -> p y q h", h=2, q=GRID // 2))
            staged[(b, oh, h)] = stage

        def store_bank(b, oh, h):
            rows = GRID // HALVES
            nc.sync.dma_start(
                out=out[b, M_TILE * oh : M_TILE * (oh + 1), rows * h : rows * (h + 1), :].rearrange(
                    "o y z -> o (y z)"
                ),
                in_=staged[(b, oh, h)][:].rearrange("p y q h -> p (y q h)"),
            )

        def empty(b):
            for oh in range(OUT_CH // M_TILE):
                for h in range(HALVES):
                    empty_bank(nc.scalar.copy, b, oh, h)

        def store(b):
            for oh in range(OUT_CH // M_TILE):
                for h in range(HALVES):
                    store_bank(b, oh, h)

        def pass_0(b, ich):
            contract(b, ich, 0, below[(b, ich)])

        def after_pass_0(b, ich):
            move_lane(below[(b, ich)], 3, above[(b, ich)], 3, 1, GRID)

        def pass_1(b, ich):
            contract(b, ich, 1, below[(b, ich)])

        def before_pass_3(b, ich):
            move_lane(above[(b, ich)], 0, below[(b, ich)], 0, 2, SIDE - 1)

        def pass_3(b, ich):
            contract(b, ich, 3, above[(b, ich)])
            move_lane(above[(b, ich)], 1, below[(b, ich)], 1, 2, GRID + 1)

        def pass_2(b, ich, part=(0, 1)):
            contract(b, ich, 2, above[(b, ich)], part)

        load_x(0)
        doubled_below[0] = doubled_tiles[0]
        double_left(nc.vector.tensor_copy, doubled_below[0], x_left[0], 0, SPLIT_ROW - 1)
        double_left(nc.scalar.copy, doubled_below[0], x_left[0], SPLIT_ROW, SIDE - 1)
        for s in range(WINDOW):
            load_left_lane(x_left_above0, 0 if s > 0 else LAST, s)
        load_x_above(0)
        scale_rows = W_scales.rearrange("g q n -> (g q) n").rearrange("(c a) n -> c (a n)", a=PASSES).bitcast(I32)
        for quadrant in range(4):
            nc.sync.dma_start(
                out=w_scales[32 * quadrant : 32 * quadrant + 4].rearrange("p a n -> p (a n)").bitcast(I32),
                in_=scale_rows[4 * quadrant : 4 * quadrant + 4, :],
            )
        load_weights(0, 0)
        load_weights(1, 0)
        load_x(1)
        load_weights(0, 1)
        load_weights(0, 3)
        first, second, third = (0,), (-1,), (1,)
        double_above(nc.scalar.copy, 0, x_left_above0)
        multiply_below(0)
        join_below(0, 0)
        join_below(0, 1)
        multiply_above(0)
        park(0)
        double_below(nc.scalar.copy, 1)
        prepare_above(1)
        pass_0(0, 0)
        join_above(0, 0, nc.vector.tensor_copy)
        after_pass_0(0, 0)
        before_pass_3(0, 0)
        pass_0(0, 1)
        join_above(0, 1)
        after_pass_0(0, 1)
        before_pass_3(0, 1)
        load_left(2)
        load_weights(1, 1)
        load_weights(1, 3)
        load_below(2)

        multiply_below(1)
        double_above(nc.scalar.copy, 1, x_left[1])
        join_below(1, 0)
        join_below(1, 1)
        pass_1(0, 0)
        pass_3(0, 0)
        load_weights(0, 2)
        multiply_above(1, first)
        multiply_above(1, second)
        pass_1(0, 1)
        multiply_above(1, third)
        park(1)
        double_below(nc.scalar.copy, 2)
        join_above(1, 0)
        pass_3(0, 1)
        before_pass_3(1, 0)
        load_weights(1, 2)
        join_above(1, 1)
        pass_0(1, 0)
        after_pass_0(1, 0)
        before_pass_3(1, 1)
        pass_2(0, 0)
        pass_0(1, 1)
        after_pass_0(1, 1)
        load_x_above(2)
        double_below(nc.scalar.copy, 3)

        multiply_below(2, first)
        pass_2(0, 1)
        empty(0)
        multiply_below(2, second)
        pass_1(1, 0)
        multiply_below(2, third)
        turn_above(2)
        join_below(2, 0)
        join_below(2, 1)
        pass_3(1, 0)
        store(0)
        pass_1(1, 1)
        pass_3(1, 1)
        load_below(3)
        multiply_above(2)
        park(2)
        join_above(2, 0)
        pass_0(2, 0)
        pass_2(1, 0)
        before_pass_3(2, 0)
        after_pass_0(2, 0)
        join_above(2, 1)
        pass_2(1, 1)
        before_pass_3(2, 1)
        pass_0(2, 1)
        after_pass_0(2, 1)
        empty(1)

        multiply_below(3)
        join_below(3, 0)
        join_above(3, 0)
        join_below(3, 1)
        pass_1(2, 0)
        pass_3(2, 0)
        pass_1(2, 1)
        pass_3(2, 1)
        join_above(3, 1)
        store(1)
        before_pass_3(3, 0)
        before_pass_3(3, 1)
        pass_0(3, 0)
        after_pass_0(3, 0)
        pass_2(2, 0)
        pass_2(2, 1)
        empty(2)
        pass_0(3, 1)
        after_pass_0(3, 1)
        pass_3(3, 0)
        store(2)
        pass_3(3, 1)
        pass_1(3, 0)
        pass_1(3, 1)
        for h in range(HALVES):
            pass_2(3, 0, (h,))
            pass_2(3, 1, (h,))
